import numpy as np
import ml_dtypes


def mxq(x, axis, fmt="e4m3"):
    dtype, down = {"e4m3": (ml_dtypes.float8_e4m3fn, 7), "e5m2": (ml_dtypes.float8_e5m2, 14)}[fmt]
    v = np.moveaxis(np.asarray(x, np.float32).astype(ml_dtypes.bfloat16).astype(np.float64), axis, -1)
    blocks = v.reshape(v.shape[:-1] + (-1, 32))
    amax = np.abs(blocks).max(-1, keepdims=True)
    byte = np.maximum(np.where(amax > 0, np.frexp(amax)[1] - 1 + 127, 0) - down, 1)
    scale = np.exp2(byte - 127.0)
    codes = (blocks / scale).astype(np.float32).astype(dtype).astype(np.float64)
    return np.moveaxis((codes * scale).reshape(v.shape), -1, axis)


WIDE = False


def mx_kscale(k):
    if not WIDE:
        return np.ones(k)
    levels = np.array([10, -10, 5, -5, 0])
    a = np.random.permutation(np.resize(levels, k // 512 * 4)).reshape(k // 512, 4)
    idx = np.arange(k)
    return np.exp2(a[idx // 512, idx % 128 // 32])


BF16 = ml_dtypes.bfloat16


def bf(x):
    return np.asarray(x, np.float32).astype(BF16)


def f64(x):
    return np.asarray(x).astype(np.float64)


E2M1 = np.array([0.0, 0.5, 1.0, 1.5, 2.0, 3.0, 4.0, 6.0, -0.0, -0.5, -1.0, -1.5, -2.0, -3.0, -4.0, -6.0])


def pack_weight(w, fmt):
    k, n = w.shape
    w = f64(bf(w)).reshape(k // 32, 32, n)
    amax = np.abs(w).max(1)
    if fmt == "e4m3":
        byte = np.frexp(amax)[1] - 1 + 127 - 7
    else:
        mant, ex = np.frexp(amax / 6.0)
        byte = np.where(mant > 0.5, ex, ex - 1) + 127
    byte = np.clip(np.where(amax > 0, byte, 1), 1, 254)
    scaled = (w * np.exp2(127.0 - byte)[:, None, :]).reshape(k, n).astype(np.float32)
    by_word = np.ascontiguousarray(scaled.reshape(k // 512, 128, 4, n).transpose(0, 1, 3, 2))
    if fmt == "e4m3":
        words = by_word.astype(ml_dtypes.float8_e4m3fn).view(np.uint8)
    else:
        c = by_word.astype(ml_dtypes.float4_e2m1fn).view(np.uint8) & 0xF
        words = c[..., 0::2] | (c[..., 1::2] << 4)
    return np.ascontiguousarray(words), np.ascontiguousarray(byte.astype(np.uint8).reshape(k // 512, 16, n))


def unpack_weight(words, scales, fmt):
    g, p, n, _ = words.shape
    if fmt == "e4m3":
        vals = np.ascontiguousarray(words).view(ml_dtypes.float8_e4m3fn).astype(np.float64)
    else:
        nib = np.empty((g, p, n, 4), np.uint8)
        nib[..., 0::2] = words & 0xF
        nib[..., 1::2] = words >> 4
        vals = E2M1[nib]
    vals = vals * np.repeat(np.exp2(scales.astype(np.float64) - 127.0), 8, axis=1)[..., None]
    return vals.transpose(0, 1, 3, 2).reshape(g * 512, n)


B, S, K, IN, HID, OUT = 4, 8, 16, 16384, 512, 511
LN_EPS = 1e-5
LINK_EPS = 1e-8
FMT = "e4m3"


def sigmoid(v):
    return 1.0 / (1.0 + np.exp(-v))


def setup_inputs():
    s, t = mx_kscale(IN), mx_kscale(HID)
    keep = np.random.random((B, S, 1, 1)) > 0.125
    net_in = bf(np.random.standard_normal((B, S, K, IN)) * s)
    embeds = bf(np.random.standard_normal((B, S, OUT)) * 0.5)
    m = bf(np.random.random((B, S, K, 1)) * keep)
    W1_words, W1_scales = pack_weight(np.random.standard_normal((IN, HID)) / np.sqrt(IN) / s[:, None] * t, FMT)
    b1 = bf(np.random.standard_normal(HID) * 0.3 * t)
    Wf_words, Wf_scales = pack_weight(np.random.standard_normal((HID, OUT + 1)) * 3.0 / np.sqrt(HID) / t[:, None], FMT)
    b_f = bf(np.random.standard_normal(OUT + 1) * 0.3)
    gamma = bf(1.0 + 0.1 * np.random.standard_normal(OUT))
    beta = bf(0.1 * np.random.standard_normal(OUT))
    return {"net_in": net_in,
            "embeds": embeds,
            "m": m,
            "W1_words": W1_words,
            "W1_scales": W1_scales,
            "b1": b1,
            "Wf_words": Wf_words,
            "Wf_scales": Wf_scales,
            "b_f": b_f,
            "gamma": gamma,
            "beta": beta}


def reference(net_in, embeds, m, W1_words, W1_scales, b1, Wf_words, Wf_scales, b_f, gamma, beta):
    h = np.maximum((mxq(f64(net_in), 3, "e4m3") @ unpack_weight(W1_words, W1_scales, FMT)) + f64(b1), 0.0)
    out = (mxq(h, 3, "e4m3") @ unpack_weight(Wf_words, Wf_scales, FMT)) + f64(b_f)
    out = np.concatenate([out[..., :-1], sigmoid(out[..., -1:])], axis=-1)
    out = f64(m) * out
    link_weight = out[..., -1] + LINK_EPS
    norm = link_weight.sum(axis=2, keepdims=True)
    weights = (link_weight / norm)[..., None]
    updates = (out * weights).sum(axis=2)
    upd_weights = updates[..., -1:]
    embeds_new = f64(embeds) + upd_weights * updates[..., :-1]
    mu = embeds_new.mean(axis=-1, keepdims=True)
    var = ((embeds_new - mu) ** 2).mean(axis=-1, keepdims=True)
    return (embeds_new - mu) / np.sqrt(var + LN_EPS) * f64(gamma) + f64(beta)

@@ -1,0 +1,353 @@
+from contextlib import ExitStack
+
+import concourse.mybir as mybir
+from concourse.masks import make_identity
+
+F32 = mybir.dt.float32
+BF16 = mybir.dt.bfloat16
+I32 = mybir.dt.int32
+U32 = mybir.dt.uint32
+U8 = mybir.dt.uint8
+FP8X4 = mybir.dt.float8_e4m3fn_x4
+ALU = mybir.AluOpType
+ACT = mybir.ActivationFunctionType
+AXIS = mybir.AxisListType
+
+P = 128
+ROWS = 512
+ROW_TILES = ROWS // P
+TOKENS = 32
+LINK_PARTS = P // TOKENS
+K_IN = 16384
+K_PASS = 512
+GROUPS = K_IN // K_PASS
+HID = 512
+CH = 512
+FEAT = CH - 1
+PAIR_WORDS = K_PASS // 2
+STEP_GROUPS = 2
+STEPS = GROUPS // STEP_GROUPS
+CHUNK_GROUPS = 4
+CHUNKS = GROUPS // CHUNK_GROUPS
+CHUNK_STEPS = CHUNK_GROUPS // STEP_GROUPS
+CHUNK_K = CHUNK_GROUPS * K_PASS
+PREFETCH = 3
+LN_EPS = 1e-5
+LINK_EPS = 1e-8
+
+FLOPS = 2 * ROWS * K_IN * HID + 2 * ROWS * HID * CH
+
+
+def tile_embed_update_pa_k_kernel(
+    tc, net_in, embeds, m, W1_words, W1_scales, b1, Wf_words, Wf_scales, b_f, gamma, beta, out
+):
+    nc = tc.nc
+    x_dram = net_in.rearrange("b s k i -> (b s k) i").rearrange("(p r) i -> p r i", r=ROW_TILES)
+    w1_dram = W1_words.rearrange("g p n t -> p g (n t)").bitcast(I32)
+
+    with ExitStack() as ctx:
+        ctx.enter_context(tc.manual_schedule())
+        consts = ctx.enter_context(tc.tile_pool(name="consts", bufs=1))
+        x_pool = ctx.enter_context(tc.tile_pool(name="x_pool", bufs=PREFETCH + 1))
+        w_pool = ctx.enter_context(tc.tile_pool(name="w_pool", bufs=PREFETCH + 1))
+        work = ctx.enter_context(tc.tile_pool(name="work", bufs=3))
+        tail = ctx.enter_context(tc.tile_pool(name="tail", bufs=1))
+        sums = ctx.enter_context(tc.psum_pool(name="sums", bufs=1))
+        banks = ctx.enter_context(tc.psum_pool(name="banks", bufs=4))
+
+        ident_f32 = consts.tile([P, P], F32)
+        make_identity(nc, ident_f32[:])
+
+        w1_planes = consts.tile([P, CHUNKS, HID], U8, align_bytes=64)
+        nc.vector.memset(w1_planes[:].bitcast(I32), 0)
+        vecs = consts.tile([P, CH], BF16)
+        nc.vector.memset(vecs[:], 0.0)
+        wf_plane = consts.tile([P, CH], U8, align_bytes=64)
+        nc.vector.memset(wf_plane[:].bitcast(I32), 0)
+        zero_col = consts.tile([P, 1], F32)
+        nc.vector.memset(zero_col[:], 0.0)
+        neg_half = consts.tile([TOKENS, 1], F32)
+        nc.vector.memset(neg_half[:], -0.5)
+        pool_w = consts.tile([P, ROW_TILES, P], F32)
+        nc.vector.memset(pool_w[:], 0.0)
+        token_of = consts.tile([P, P], F32)
+        nc.vector.memset(token_of[:], 0.0)
+
+        nc.scalar.dma_start(out=vecs[0:1, 0:HID], in_=b1.rearrange("(o n) -> o n", o=1))
+        nc.scalar.dma_start(out=vecs[1:2, 0:CH], in_=b_f.rearrange("(o n) -> o n", o=1))
+        nc.scalar.dma_start(out=vecs[2:3, 0:FEAT], in_=gamma.rearrange("(o n) -> o n", o=1))
+        nc.scalar.dma_start(out=vecs[3:4, 0:FEAT], in_=beta.rearrange("(o n) -> o n", o=1))
+        m_bf = consts.tile([P, ROW_TILES], BF16)
+        nc.scalar.dma_start(
+            out=m_bf[:], in_=m.rearrange("b s k o -> (b s k o)").rearrange("(p r) -> p r", r=ROW_TILES)
+        )
+        emb = consts.tile([TOKENS, FEAT], BF16)
+        nc.scalar.dma_start(out=emb[:], in_=embeds.rearrange("b s c -> (b s) c"))
+
+        warm = consts.tile([P, 1], F32)
+        nc.scalar.activation(out=warm[:], in_=zero_col[:], func=ACT.Sigmoid)
+
+        x_tiles = {}
+        w_tiles = {}
+
+        def load_chunk(c):
+            x_raw = x_pool.tile([P, ROW_TILES, CHUNK_K], BF16, name="x_raw")
+            pieces = CHUNK_STEPS if c == 0 else 1
+            width = CHUNK_K // pieces
+            for h in range(pieces):
+                nc.sync.dma_start(
+                    out=x_raw[:, :, h * width : (h + 1) * width],
+                    in_=x_dram[:, :, c * CHUNK_K + h * width : c * CHUNK_K + (h + 1) * width],
+                )
+            for q in range(4):
+                nc.sync.dma_start(
+                    out=w1_planes[32 * q : 32 * q + 16, c, :].bitcast(I32),
+                    in_=W1_scales[
+                        c * CHUNK_GROUPS : (c + 1) * CHUNK_GROUPS, 4 * q : 4 * q + 4, :
+                    ].bitcast(I32),
+                )
+            w_words = w_pool.tile([P, CHUNK_GROUPS, HID], U32, name="w_words", align_bytes=64)
+            nc.sync.dma_start(
+                out=w_words[:].bitcast(I32),
+                in_=w1_dram[:, c * CHUNK_GROUPS : (c + 1) * CHUNK_GROUPS, :],
+            )
+            x_tiles[c] = x_raw
+            w_tiles[c] = w_words
+
+        for c in range(PREFETCH):
+            load_chunk(c)
+
+        ident_bf = consts.tile([P, P], BF16)
+        nc.vector.tensor_copy(out=ident_bf[:], in_=ident_f32[:])
+        nc.vector.tensor_reduce(
+            out=token_of[:, 0:TOKENS],
+            in_=ident_f32[:].rearrange("p (j i) -> p j i", i=LINK_PARTS),
+            axis=AXIS.X,
+            op=ALU.add,
+        )
+        m_f32 = consts.tile([P, ROW_TILES], F32)
+        nc.vector.tensor_copy(out=m_f32[:], in_=m_bf[:])
+
+        spread = []
+        for j in range(4):
+            picked = sums.tile([P, CH], F32, name="picked", tag="sum%d" % j)
+            nc.tensor.matmul(
+                out=picked[:],
+                lhsT=ident_bf[:, j : j + 1].to_broadcast([P, P]),
+                rhs=vecs[:],
+                start=True,
+                stop=True,
+            )
+            row = consts.tile([P, CH], F32, name="spread%d" % j)
+            nc.scalar.copy(out=row[:], in_=picked[:])
+            spread.append(row)
+        b1_all, bf_all, gamma_all, beta_all = spread
+
+        acc = [sums.tile([P, HID], F32, name="acc%d" % r, tag="sum%d" % r) for r in range(ROW_TILES)]
+        sorted_tiles = {}
+        grouped_tiles = {}
+
+        def sort_step(i):
+            c, h = divmod(i, CHUNK_STEPS)
+            words = x_tiles[c][:].bitcast(F32)
+            first = h * STEP_GROUPS * PAIR_WORDS
+            x_sorted = work.tile([P, ROW_TILES, 2, STEP_GROUPS * P], F32, name="x_sorted")
+            nc.vector.tensor_copy(
+                out=x_sorted[:],
+                in_=words[:, :, first : first + STEP_GROUPS * PAIR_WORDS].rearrange(
+                    "p r (q u) -> p r u q", u=2
+                ),
+            )
+            sorted_tiles[i] = x_sorted
+
+        def transpose_step(i):
+            x_sorted = sorted_tiles[i]
+            grouped = work.tile([P, STEP_GROUPS, 4 * ROWS], BF16, name="grouped", align_bytes=64)
+            grouped_words = grouped[:].bitcast(F32)
+            for g in range(STEP_GROUPS):
+                for half in range(2):
+                    bank = banks.tile([P, 4 * P], F32, name="bank")
+                    for r2 in range(2):
+                        for u in range(2):
+                            nc.tensor.transpose(
+                                bank[:, (2 * r2 + u) * P : (2 * r2 + u + 1) * P],
+                                x_sorted[:, 2 * half + r2, u, g * P : (g + 1) * P],
+                                ident_f32[:],
+                            )
+                    nc.scalar.copy(
+                        out=grouped_words[:, g, half * 4 * P : (half + 1) * 4 * P].rearrange(
+                            "p (r j u) -> p r j u", r=2, u=2
+                        ),
+                        in_=bank[:].rearrange("p (r u j) -> p r j u", r=2, u=2),
+                    )
+            grouped_tiles[i] = grouped
+
+        def multiply_step(i):
+            grouped = grouped_tiles[i]
+            x_codes = work.tile([P, STEP_GROUPS, ROWS], U32, name="x_codes", align_bytes=64)
+            x_planes = work.tile([P, STEP_GROUPS, ROWS], U8, name="x_planes", align_bytes=64)
+            for g in range(STEP_GROUPS):
+                nc.vector.quantize_mx(
+                    out=x_codes[:, g, :].bitcast(FP8X4), scales=x_planes[:, g, :], in_=grouped[:, g, :]
+                )
+            c, h = divmod(i, CHUNK_STEPS)
+            for r in range(ROW_TILES):
+                for g in range(STEP_GROUPS):
+                    j = h * STEP_GROUPS + g
+                    group = i * STEP_GROUPS + g
+                    nc.tensor.matmul_mx(
+                        out=acc[r][:],
+                        lhsT=x_codes[:, g, r * P : (r + 1) * P].bitcast(FP8X4),
+                        lhsT_scale=x_planes[:, g, r * P : (r + 1) * P],
+                        rhs=w_tiles[c][:, j, :].bitcast(FP8X4),
+                        rhs_scale=w1_planes[4 * j : P, c, :],
+                        start=(group == 0),
+                        stop=(group == GROUPS - 1),
+                    )
+
+        sort_step(0)
+        for i in range(STEPS):
+            transpose_step(i)
+            if i >= 1:
+                multiply_step(i - 1)
+            if i + 1 < STEPS:
+                sort_step(i + 1)
+            c, h = divmod(i, CHUNK_STEPS)
+            if h == 0 and c + PREFETCH < CHUNKS:
+                load_chunk(c + PREFETCH)
+        multiply_step(STEPS - 1)
+
+        wf_words = consts.tile([P, CH], U32, align_bytes=64)
+        nc.sync.dma_start(
+            out=wf_words[:].bitcast(I32), in_=Wf_words[0].rearrange("p n t -> p (n t)").bitcast(I32)
+        )
+        for q in range(4):
+            nc.sync.dma_start(
+                out=wf_plane[32 * q : 32 * q + 4, :].bitcast(I32),
+                in_=Wf_scales[0, 4 * q : 4 * q + 4, :].bitcast(I32),
+            )
+
+        pre_h = tail.tile([P, ROW_TILES, HID], BF16)
+        for r in range(ROW_TILES):
+            nc.vector.tensor_tensor(out=pre_h[:, r, :], in0=acc[r][:], in1=b1_all[:], op=ALU.add)
+        pre_h_words = pre_h[:].bitcast(F32)
+        h_grouped = tail.tile([P, ROW_TILES, HID], BF16, align_bytes=64)
+        for r in range(ROW_TILES):
+            bank = banks.tile([P, 4 * P], F32, name="bank")
+            for u in range(2):
+                nc.tensor.transpose(
+                    bank[:, u * P : (u + 1) * P], pre_h_words[:, r, u : PAIR_WORDS : 2], ident_f32[:]
+                )
+            nc.scalar.activation(
+                out=h_grouped[:, r, :].rearrange("p (j u e) -> p j u e", u=2, e=2),
+                in_=bank[:, 0 : 2 * P].bitcast(BF16).rearrange("p (u j e) -> p j u e", u=2, e=2),
+                func=ACT.Relu,
+            )
+        h_codes = tail.tile([P, ROW_TILES, P], U32, align_bytes=64)
+        h_planes = tail.tile([P, ROW_TILES, P], U8, align_bytes=64)
+        o_sum = []
+        for r in range(ROW_TILES):
+            nc.vector.quantize_mx(
+                out=h_codes[:, r, :].bitcast(FP8X4), scales=h_planes[:, r, :], in_=h_grouped[:, r, :]
+            )
+            o_ps = sums.tile([P, CH], F32, name="o_ps", tag="sum%d" % r)
+            nc.tensor.matmul_mx(
+                out=o_ps[:],
+                lhsT=h_codes[:, r, :].bitcast(FP8X4),
+                lhsT_scale=h_planes[:, r, :],
+                rhs=wf_words[:].bitcast(FP8X4),
+                rhs_scale=wf_plane[:],
+                start=True,
+                stop=True,
+            )
+            o_sum.append(o_ps)
+
+        o_sb = tail.tile([P, ROW_TILES, CH], F32)
+        link_w = tail.tile([P, ROW_TILES], F32)
+        pooled = banks.tile([P, CH], F32, name="bank")
+        link_sum = banks.tile([P, 4 * P], F32, name="bank")
+
+        def score_links(r):
+            nc.vector.tensor_tensor(out=o_sb[:, r, :], in0=o_sum[r][:], in1=bf_all[:], op=ALU.add)
+            nc.scalar.activation(out=o_sb[:, r, FEAT:CH], in_=o_sb[:, r, FEAT:CH], func=ACT.Sigmoid)
+
+        def pool_links(r):
+            nc.vector.tensor_scalar(
+                out=link_w[:, r : r + 1],
+                in0=o_sb[:, r, FEAT:CH],
+                scalar1=m_f32[:, r : r + 1],
+                scalar2=LINK_EPS,
+                op0=ALU.mult,
+                op1=ALU.add,
+            )
+            nc.vector.tensor_scalar(
+                out=pool_w[:, r, 0:TOKENS],
+                in0=token_of[:, 0:TOKENS],
+                scalar1=link_w[:, r : r + 1],
+                scalar2=m_f32[:, r : r + 1],
+                op0=ALU.mult,
+                op1=ALU.mult,
+            )
+            nc.tensor.matmul(
+                out=pooled[:],
+                lhsT=pool_w[:, r, :],
+                rhs=o_sb[:, r, :],
+                start=(r == 0),
+                stop=(r == ROW_TILES - 1),
+            )
+
+        for r in range(ROW_TILES):
+            score_links(r)
+            if r >= 1:
+                pool_links(r - 1)
+        pool_links(ROW_TILES - 1)
+        nc.tensor.matmul(
+            out=link_sum[:, 0:ROW_TILES], lhsT=token_of[:], rhs=link_w[:], start=True, stop=True
+        )
+
+        total = tail.tile([TOKENS, 1], F32)
+        nc.vector.tensor_reduce(
+            out=total[:], in_=link_sum[0:TOKENS, 0:ROW_TILES], axis=AXIS.X, op=ALU.add
+        )
+        inv = tail.tile([TOKENS, 1], F32)
+        nc.vector.reciprocal(out=inv[:], in_=total[:])
+        gain = tail.tile([TOKENS, 1], F32)
+        nc.vector.tensor_scalar(
+            out=gain[:],
+            in0=pooled[0:TOKENS, FEAT:CH],
+            scalar1=inv[:],
+            scalar2=inv[:],
+            op0=ALU.mult,
+            op1=ALU.mult,
+        )
+        e = tail.tile([TOKENS, FEAT], F32)
+        nc.vector.scalar_tensor_tensor(
+            out=e[:], in0=pooled[0:TOKENS, 0:FEAT], scalar=gain[:], in1=emb[:], op0=ALU.mult, op1=ALU.add
+        )
+        stats = tail.tile([TOKENS, 6], F32)
+        nc.vector.bn_stats(out=stats[:], in_=e[:])
+        mean_var = tail.tile([TOKENS, 2], F32)
+        nc.vector.bn_aggr(out=mean_var[:], in_=stats[:])
+        var_eps = tail.tile([TOKENS, 1], F32)
+        nc.vector.tensor_scalar_add(out=var_eps[:], in0=mean_var[:, 1:2], scalar1=LN_EPS)
+        rstd = tail.tile([TOKENS, 1], F32)
+        nc.gpsimd.tensor_tensor(out=rstd[:], in0=var_eps[:], in1=neg_half[:], op=ALU.pow)
+        centred = tail.tile([TOKENS, FEAT], F32)
+        nc.vector.scalar_tensor_tensor(
+            out=centred[:],
+            in0=e[:],
+            scalar=mean_var[:, 0:1],
+            in1=gamma_all[0:TOKENS, 0:FEAT],
+            op0=ALU.subtract,
+            op1=ALU.mult,
+        )
+        y = tail.tile([TOKENS, FEAT], F32)
+        nc.vector.scalar_tensor_tensor(
+            out=y[:],
+            in0=centred[:],
+            scalar=rstd[:],
+            in1=beta_all[0:TOKENS, 0:FEAT],
+            op0=ALU.mult,
+            op1=ALU.add,
+        )
+        nc.sync.dma_start(out=out.rearrange("b s c -> (b s) c"), in_=y[:])

@@ -25,13 +25,20 @@ HID = 512
 CH = 512
 FEAT = CH - 1
 PAIR_WORDS = K_PASS // 2
-STEP_GROUPS = 2
-STEPS = GROUPS // STEP_GROUPS
+UNITS = 8
+CALL_UNITS = 4
 CHUNK_GROUPS = 4
 CHUNKS = GROUPS // CHUNK_GROUPS
+LAST_GROUPS = UNITS
+JOINT_GROUPS = GROUPS - LAST_GROUPS
+JOINT_CHUNKS = JOINT_GROUPS // CHUNK_GROUPS
+STEP_GROUPS = UNITS // ROW_TILES
+JOINT_STEPS = JOINT_GROUPS // STEP_GROUPS
+STEPS = JOINT_STEPS + ROW_TILES
 CHUNK_STEPS = CHUNK_GROUPS // STEP_GROUPS
 CHUNK_K = CHUNK_GROUPS * K_PASS
-PREFETCH = 3
+X_BUFS = 4
+W_BUFS = 6
 LN_EPS = 1e-5
 LINK_EPS = 1e-8
 
@@ -48,30 +55,28 @@ def tile_embed_update_pa_k_kernel(
     with ExitStack() as ctx:
         ctx.enter_context(tc.manual_schedule())
         consts = ctx.enter_context(tc.tile_pool(name="consts", bufs=1))
-        x_pool = ctx.enter_context(tc.tile_pool(name="x_pool", bufs=PREFETCH + 1))
-        w_pool = ctx.enter_context(tc.tile_pool(name="w_pool", bufs=PREFETCH + 1))
-        work = ctx.enter_context(tc.tile_pool(name="work", bufs=3))
+        x_pool = ctx.enter_context(tc.tile_pool(name="x_pool", bufs=X_BUFS))
+        w_pool = ctx.enter_context(tc.tile_pool(name="w_pool", bufs=W_BUFS))
+        work = ctx.enter_context(tc.tile_pool(name="work", bufs=2))
         tail = ctx.enter_context(tc.tile_pool(name="tail", bufs=1))
         sums = ctx.enter_context(tc.psum_pool(name="sums", bufs=1))
         banks = ctx.enter_context(tc.psum_pool(name="banks", bufs=4))
 
-        ident_f32 = consts.tile([P, P], F32)
-        make_identity(nc, ident_f32[:])
-
-        w1_planes = consts.tile([P, CHUNKS, HID], U8, align_bytes=64)
-        nc.vector.memset(w1_planes[:].bitcast(I32), 0)
         vecs = consts.tile([P, CH], BF16)
         nc.vector.memset(vecs[:], 0.0)
-        wf_plane = consts.tile([P, CH], U8, align_bytes=64)
-        nc.vector.memset(wf_plane[:].bitcast(I32), 0)
+        w1_planes = consts.tile([P, CHUNKS, HID], U8, align_bytes=64)
+        nc.vector.memset(w1_planes[:, 0, :].bitcast(I32), 0)
         zero_col = consts.tile([P, 1], F32)
         nc.vector.memset(zero_col[:], 0.0)
-        neg_half = consts.tile([TOKENS, 1], F32)
-        nc.vector.memset(neg_half[:], -0.5)
-        pool_w = consts.tile([P, ROW_TILES, P], F32)
-        nc.vector.memset(pool_w[:], 0.0)
+        nc.vector.memset(w1_planes[:, 1:CHUNKS, :].bitcast(I32), 0)
+        ident_f32 = consts.tile([P, P], F32)
+        make_identity(nc, ident_f32[:])
+        wf_plane = consts.tile([P, CH], U8, align_bytes=64)
+        nc.gpsimd.memset(wf_plane[:].bitcast(I32), 0)
         token_of = consts.tile([P, P], F32)
-        nc.vector.memset(token_of[:], 0.0)
+        nc.gpsimd.memset(token_of[:], 0.0)
+        neg_half = consts.tile([TOKENS, 1], F32)
+        nc.gpsimd.memset(neg_half[:], -0.5)
 
         nc.scalar.dma_start(out=vecs[0:1, 0:HID], in_=b1.rearrange("(o n) -> o n", o=1))
         nc.scalar.dma_start(out=vecs[1:2, 0:CH], in_=b_f.rearrange("(o n) -> o n", o=1))
@@ -90,15 +95,24 @@ def tile_embed_update_pa_k_kernel(
         x_tiles = {}
         w_tiles = {}
 
-        def load_chunk(c):
+        def load_x(c, pieces):
             x_raw = x_pool.tile([P, ROW_TILES, CHUNK_K], BF16, name="x_raw")
-            pieces = CHUNK_STEPS if c == 0 else 1
-            width = CHUNK_K // pieces
-            for h in range(pieces):
+            first = 0
+            for groups in pieces:
+                last = first + groups * K_PASS
                 nc.sync.dma_start(
-                    out=x_raw[:, :, h * width : (h + 1) * width],
-                    in_=x_dram[:, :, c * CHUNK_K + h * width : c * CHUNK_K + (h + 1) * width],
+                    out=x_raw[:, :, first:last],
+                    in_=x_dram[:, :, c * CHUNK_K + first : c * CHUNK_K + last],
                 )
+                first = last
+            x_tiles[c] = x_raw
+
+        def load_x_last(r):
+            x_last = consts.tile([P, LAST_GROUPS * K_PASS], BF16, name="x_last%d" % r)
+            nc.sync.dma_start(out=x_last[:], in_=x_dram[:, r, JOINT_GROUPS * K_PASS : K_IN])
+            x_tiles[JOINT_CHUNKS + r] = x_last
+
+        def load_w(c):
             for q in range(4):
                 nc.sync.dma_start(
                     out=w1_planes[32 * q : 32 * q + 16, c, :].bitcast(I32),
@@ -111,11 +125,13 @@ def tile_embed_update_pa_k_kernel(
                 out=w_words[:].bitcast(I32),
                 in_=w1_dram[:, c * CHUNK_GROUPS : (c + 1) * CHUNK_GROUPS, :],
             )
-            x_tiles[c] = x_raw
             w_tiles[c] = w_words
 
-        for c in range(PREFETCH):
-            load_chunk(c)
+        load_x(0, [1, 1, 2])
+        load_w(0)
+        for c in range(1, X_BUFS):
+            load_x(c, [CHUNK_GROUPS])
+            load_w(c)
 
         ident_bf = consts.tile([P, P], BF16)
         nc.vector.tensor_copy(out=ident_bf[:], in_=ident_f32[:])
@@ -125,9 +141,6 @@ def tile_embed_update_pa_k_kernel(
             axis=AXIS.X,
             op=ALU.add,
         )
-        m_f32 = consts.tile([P, ROW_TILES], F32)
-        nc.vector.tensor_copy(out=m_f32[:], in_=m_bf[:])
-
         spread = []
         for j in range(4):
             picked = sums.tile([P, CH], F32, name="picked", tag="sum%d" % j)
@@ -147,92 +160,97 @@ def tile_embed_update_pa_k_kernel(
         sorted_tiles = {}
         grouped_tiles = {}
 
+        def units_of(i):
+            if i < JOINT_STEPS:
+                return [(r, STEP_GROUPS * i + g) for g in range(STEP_GROUPS) for r in range(ROW_TILES)]
+            return [(i - JOINT_STEPS, JOINT_GROUPS + g) for g in range(LAST_GROUPS)]
+
         def sort_step(i):
-            c, h = divmod(i, CHUNK_STEPS)
-            words = x_tiles[c][:].bitcast(F32)
-            first = h * STEP_GROUPS * PAIR_WORDS
-            x_sorted = work.tile([P, ROW_TILES, 2, STEP_GROUPS * P], F32, name="x_sorted")
-            nc.vector.tensor_copy(
-                out=x_sorted[:],
-                in_=words[:, :, first : first + STEP_GROUPS * PAIR_WORDS].rearrange(
-                    "p r (q u) -> p r u q", u=2
-                ),
-            )
+            x_sorted = work.tile([P, UNITS, 2, P], F32, name="x_sorted")
+            if i < JOINT_STEPS:
+                c, h = divmod(i, CHUNK_STEPS)
+                words = x_tiles[c][:].bitcast(F32)
+                for g in range(STEP_GROUPS):
+                    first = (h * STEP_GROUPS + g) * PAIR_WORDS
+                    nc.vector.tensor_copy(
+                        out=x_sorted[:, g * ROW_TILES : (g + 1) * ROW_TILES, :, :],
+                        in_=words[:, :, first : first + PAIR_WORDS].rearrange(
+                            "p r (q u) -> p r u q", u=2
+                        ),
+                    )
+            else:
+                words = x_tiles[JOINT_CHUNKS + i - JOINT_STEPS][:].bitcast(F32)
+                nc.vector.tensor_copy(
+                    out=x_sorted[:], in_=words.rearrange("p (k q u) -> p k u q", u=2, q=P)
+                )
             sorted_tiles[i] = x_sorted
 
         def transpose_step(i):
             x_sorted = sorted_tiles[i]
-            grouped = work.tile([P, STEP_GROUPS, 4 * ROWS], BF16, name="grouped", align_bytes=64)
+            grouped = work.tile([P, UNITS, K_PASS], BF16, name="grouped", align_bytes=64)
             grouped_words = grouped[:].bitcast(F32)
-            for g in range(STEP_GROUPS):
-                for half in range(2):
-                    bank = banks.tile([P, 4 * P], F32, name="bank")
-                    for r2 in range(2):
-                        for u in range(2):
-                            nc.tensor.transpose(
-                                bank[:, (2 * r2 + u) * P : (2 * r2 + u + 1) * P],
-                                x_sorted[:, 2 * half + r2, u, g * P : (g + 1) * P],
-                                ident_f32[:],
-                            )
-                    nc.scalar.copy(
-                        out=grouped_words[:, g, half * 4 * P : (half + 1) * 4 * P].rearrange(
-                            "p (r j u) -> p r j u", r=2, u=2
-                        ),
-                        in_=bank[:].rearrange("p (r u j) -> p r j u", r=2, u=2),
-                    )
+            for k in range(0, UNITS, 2):
+                bank = banks.tile([P, 4 * P], F32, name="bank")
+                for k2 in range(2):
+                    for u in range(2):
+                        nc.tensor.transpose(
+                            bank[:, (2 * k2 + u) * P : (2 * k2 + u + 1) * P],
+                            x_sorted[:, k + k2, u, :],
+                            ident_f32[:],
+                        )
+                nc.scalar.copy(
+                    out=grouped_words[:, k : k + 2, :].rearrange("p k (j u) -> p k j u", u=2),
+                    in_=bank[:].rearrange("p (k u j) -> p k j u", k=2, u=2),
+                )
             grouped_tiles[i] = grouped
 
-        def multiply_step(i):
-            grouped = grouped_tiles[i]
-            x_codes = work.tile([P, STEP_GROUPS, ROWS], U32, name="x_codes", align_bytes=64)
-            x_planes = work.tile([P, STEP_GROUPS, ROWS], U8, name="x_planes", align_bytes=64)
-            for g in range(STEP_GROUPS):
-                nc.vector.quantize_mx(
-                    out=x_codes[:, g, :].bitcast(FP8X4), scales=x_planes[:, g, :], in_=grouped[:, g, :]
-                )
-            c, h = divmod(i, CHUNK_STEPS)
-            for r in range(ROW_TILES):
-                for g in range(STEP_GROUPS):
-                    j = h * STEP_GROUPS + g
-                    group = i * STEP_GROUPS + g
-                    nc.tensor.matmul_mx(
-                        out=acc[r][:],
-                        lhsT=x_codes[:, g, r * P : (r + 1) * P].bitcast(FP8X4),
-                        lhsT_scale=x_planes[:, g, r * P : (r + 1) * P],
-                        rhs=w_tiles[c][:, j, :].bitcast(FP8X4),
-                        rhs_scale=w1_planes[4 * j : P, c, :],
-                        start=(group == 0),
-                        stop=(group == GROUPS - 1),
-                    )
+        code_tiles = {}
 
-        sort_step(0)
-        for i in range(STEPS):
-            transpose_step(i)
-            if i >= 1:
-                multiply_step(i - 1)
-            if i + 1 < STEPS:
-                sort_step(i + 1)
-            c, h = divmod(i, CHUNK_STEPS)
-            if h == 0 and c + PREFETCH < CHUNKS:
-                load_chunk(c + PREFETCH)
-        multiply_step(STEPS - 1)
-
-        wf_words = consts.tile([P, CH], U32, align_bytes=64)
-        nc.sync.dma_start(
-            out=wf_words[:].bitcast(I32), in_=Wf_words[0].rearrange("p n t -> p (n t)").bitcast(I32)
-        )
-        for q in range(4):
-            nc.sync.dma_start(
-                out=wf_plane[32 * q : 32 * q + 4, :].bitcast(I32),
-                in_=Wf_scales[0, 4 * q : 4 * q + 4, :].bitcast(I32),
+        def quantise_step(i, part):
+            if part == 0:
+                x_codes = work.tile([P, UNITS, P], U32, name="x_codes", align_bytes=64)
+                x_planes = work.tile([P, UNITS, P], U8, name="x_planes", align_bytes=64)
+                code_tiles[i] = (x_codes, x_planes)
+            x_codes, x_planes = code_tiles[i]
+            units = slice(part * CALL_UNITS, (part + 1) * CALL_UNITS)
+            nc.vector.quantize_mx(
+                out=x_codes[:, units, :].rearrange("p k j -> p (k j)").bitcast(FP8X4),
+                scales=x_planes[:, units, :].rearrange("p k j -> p (k j)"),
+                in_=grouped_tiles[i][:, units, :].rearrange("p k j -> p (k j)"),
             )
 
+        def multiply_step(i):
+            x_codes, x_planes = code_tiles[i]
+            for k, (r, group) in enumerate(units_of(i)):
+                c, j = divmod(group, CHUNK_GROUPS)
+                nc.tensor.matmul_mx(
+                    out=acc[r][:],
+                    lhsT=x_codes[:, k, :].bitcast(FP8X4),
+                    lhsT_scale=x_planes[:, k, :],
+                    rhs=w_tiles[c][:, j, :].bitcast(FP8X4),
+                    rhs_scale=w1_planes[4 * j : P, c, :],
+                    start=(group == 0),
+                    stop=(group == GROUPS - 1),
+                )
+
+        wf_words = consts.tile([P, CH], U32, align_bytes=64)
         pre_h = tail.tile([P, ROW_TILES, HID], BF16)
-        for r in range(ROW_TILES):
-            nc.vector.tensor_tensor(out=pre_h[:, r, :], in0=acc[r][:], in1=b1_all[:], op=ALU.add)
-        pre_h_words = pre_h[:].bitcast(F32)
         h_grouped = tail.tile([P, ROW_TILES, HID], BF16, align_bytes=64)
-        for r in range(ROW_TILES):
+        h_codes = tail.tile([P, ROW_TILES, P], U32, align_bytes=64)
+        h_planes = tail.tile([P, ROW_TILES, P], U8, align_bytes=64)
+        gate = tail.tile([P, ROW_TILES], F32)
+        link_cols = tail.tile([P, ROW_TILES, 3], F32)
+        weighted = tail.tile([P, ROW_TILES, FEAT], F32)
+        m_f32 = consts.tile([P, ROW_TILES], F32)
+        m_sq = consts.tile([P, ROW_TILES], F32)
+        m_eps = consts.tile([P, ROW_TILES], F32)
+        o_sum = {}
+
+        def add_bias(r):
+            nc.vector.tensor_tensor(out=pre_h[:, r, :], in0=acc[r][:], in1=b1_all[:], op=ALU.add)
+
+        def transpose_hidden(r):
+            pre_h_words = pre_h[:].bitcast(F32)
             bank = banks.tile([P, 4 * P], F32, name="bank")
             for u in range(2):
                 nc.tensor.transpose(
@@ -243,13 +261,13 @@ def tile_embed_update_pa_k_kernel(
                 in_=bank[:, 0 : 2 * P].bitcast(BF16).rearrange("p (u j e) -> p j u e", u=2, e=2),
                 func=ACT.Relu,
             )
-        h_codes = tail.tile([P, ROW_TILES, P], U32, align_bytes=64)
-        h_planes = tail.tile([P, ROW_TILES, P], U8, align_bytes=64)
-        o_sum = []
-        for r in range(ROW_TILES):
+
+        def quantise_hidden(r):
             nc.vector.quantize_mx(
                 out=h_codes[:, r, :].bitcast(FP8X4), scales=h_planes[:, r, :], in_=h_grouped[:, r, :]
             )
+
+        def multiply_hidden(r):
             o_ps = sums.tile([P, CH], F32, name="o_ps", tag="sum%d" % r)
             nc.tensor.matmul_mx(
                 out=o_ps[:],
@@ -260,69 +278,158 @@ def tile_embed_update_pa_k_kernel(
                 start=True,
                 stop=True,
             )
-            o_sum.append(o_ps)
+            nc.scalar.activation(
+                out=gate[:, r : r + 1],
+                in_=o_ps[:, FEAT:CH],
+                func=ACT.Sigmoid,
+                bias=bf_all[:, FEAT:CH],
+            )
+            o_sum[r] = o_ps
 
-        o_sb = tail.tile([P, ROW_TILES, CH], F32)
-        link_w = tail.tile([P, ROW_TILES], F32)
-        pooled = banks.tile([P, CH], F32, name="bank")
-        link_sum = banks.tile([P, 4 * P], F32, name="bank")
-
-        def score_links(r):
-            nc.vector.tensor_tensor(out=o_sb[:, r, :], in0=o_sum[r][:], in1=bf_all[:], op=ALU.add)
-            nc.scalar.activation(out=o_sb[:, r, FEAT:CH], in_=o_sb[:, r, FEAT:CH], func=ACT.Sigmoid)
-
-        def pool_links(r):
+        def weigh_links(r):
+            s = gate[:, r : r + 1]
             nc.vector.tensor_scalar(
-                out=link_w[:, r : r + 1],
-                in0=o_sb[:, r, FEAT:CH],
+                out=link_cols[:, r, 1:2],
+                in0=s,
+                scalar1=m_sq[:, r : r + 1],
+                scalar2=m_eps[:, r : r + 1],
+                op0=ALU.mult,
+                op1=ALU.add,
+            )
+            if r == 0:
+                nc.vector.tensor_scalar(
+                    out=weighted[:, r, :],
+                    in0=o_sum[r][:, 0:FEAT],
+                    scalar1=link_cols[:, r, 1:2],
+                    scalar2=None,
+                    op0=ALU.mult,
+                )
+            else:
+                nc.vector.scalar_tensor_tensor(
+                    out=weighted[:, r, :],
+                    in0=o_sum[r][:, 0:FEAT],
+                    scalar=link_cols[:, r, 1:2],
+                    in1=weighted[:, r - 1, :],
+                    op0=ALU.mult,
+                    op1=ALU.add,
+                )
+            nc.vector.tensor_scalar(
+                out=link_cols[:, r, 0:1],
+                in0=s,
                 scalar1=m_f32[:, r : r + 1],
                 scalar2=LINK_EPS,
                 op0=ALU.mult,
                 op1=ALU.add,
             )
-            nc.vector.tensor_scalar(
-                out=pool_w[:, r, 0:TOKENS],
-                in0=token_of[:, 0:TOKENS],
-                scalar1=link_w[:, r : r + 1],
-                scalar2=m_f32[:, r : r + 1],
-                op0=ALU.mult,
-                op1=ALU.mult,
+            nc.vector.tensor_tensor(
+                out=link_cols[:, r, 2:3], in0=link_cols[:, r, 1:2], in1=s, op=ALU.mult
             )
+
+        sort_step(0)
+        for i in range(STEPS):
+            done = i - 2 - JOINT_STEPS
+            transpose_step(i)
+            if i >= 1:
+                quantise_step(i - 1, 0)
+                if done >= 1:
+                    quantise_hidden(done - 1)
+                quantise_step(i - 1, 1)
+            if done >= 0:
+                add_bias(done)
+                transpose_hidden(done)
+            if i >= 1:
+                multiply_step(i - 1)
+            if done >= 1:
+                multiply_hidden(done - 1)
+            if i + 1 < STEPS:
+                sort_step(i + 1)
+
+            if i == 0:
+                load_x(X_BUFS, [CHUNK_GROUPS])
+                load_w(X_BUFS)
+            if i == 2:
+                load_x(X_BUFS + 1, [CHUNK_GROUPS])
+                load_w(X_BUFS + 1)
+                nc.vector.tensor_copy(out=m_f32[:], in_=m_bf[:])
+                nc.vector.tensor_tensor(out=m_sq[:], in0=m_f32[:], in1=m_f32[:], op=ALU.mult)
+                nc.vector.tensor_scalar(
+                    out=m_eps[:], in0=m_f32[:], scalar1=LINK_EPS, scalar2=None, op0=ALU.mult
+                )
+            if i == 4:
+                load_x_last(0)
+                load_w(JOINT_CHUNKS)
+                load_w(JOINT_CHUNKS + 1)
+                for q in range(4):
+                    nc.sync.dma_start(
+                        out=wf_plane[32 * q : 32 * q + 4, :].bitcast(I32),
+                        in_=Wf_scales[0, 4 * q : 4 * q + 4, :].bitcast(I32),
+                    )
+                nc.sync.dma_start(
+                    out=wf_words[:].bitcast(I32),
+                    in_=Wf_words[0].rearrange("p n t -> p (n t)").bitcast(I32),
+                )
+                for r in range(1, ROW_TILES):
+                    load_x_last(r)
+
+        quantise_step(STEPS - 1, 0)
+        quantise_hidden(1)
+        quantise_step(STEPS - 1, 1)
+        multiply_hidden(1)
+        add_bias(2)
+        weigh_links(0)
+        weigh_links(1)
+        multiply_step(STEPS - 1)
+        transpose_hidden(2)
+        add_bias(3)
+        transpose_hidden(3)
+        quantise_hidden(2)
+        multiply_hidden(2)
+        quantise_hidden(3)
+        multiply_hidden(3)
+        weigh_links(2)
+        weigh_links(3)
+
+        link_sum = banks.tile([P, 4 * P], F32, name="bank")
+        for r in range(ROW_TILES):
             nc.tensor.matmul(
-                out=pooled[:],
-                lhsT=pool_w[:, r, :],
-                rhs=o_sb[:, r, :],
+                out=link_sum[:, 0:3],
+                lhsT=token_of[:],
+                rhs=link_cols[:, r, :],
                 start=(r == 0),
                 stop=(r == ROW_TILES - 1),
             )
-
-        for r in range(ROW_TILES):
-            score_links(r)
-            if r >= 1:
-                pool_links(r - 1)
-        pool_links(ROW_TILES - 1)
+        pooled = banks.tile([P, 4 * P], F32, name="bank")
         nc.tensor.matmul(
-            out=link_sum[:, 0:ROW_TILES], lhsT=token_of[:], rhs=link_w[:], start=True, stop=True
+            out=pooled[:, 0:FEAT], lhsT=token_of[:], rhs=weighted[:, ROW_TILES - 1, :], start=True, stop=True
         )
 
-        total = tail.tile([TOKENS, 1], F32)
-        nc.vector.tensor_reduce(
-            out=total[:], in_=link_sum[0:TOKENS, 0:ROW_TILES], axis=AXIS.X, op=ALU.add
-        )
         inv = tail.tile([TOKENS, 1], F32)
-        nc.vector.reciprocal(out=inv[:], in_=total[:])
+        nc.vector.reciprocal(out=inv[:], in_=link_sum[0:TOKENS, 0:1])
         gain = tail.tile([TOKENS, 1], F32)
         nc.vector.tensor_scalar(
             out=gain[:],
-            in0=pooled[0:TOKENS, FEAT:CH],
+            in0=link_sum[0:TOKENS, 2:3],
             scalar1=inv[:],
             scalar2=inv[:],
             op0=ALU.mult,
             op1=ALU.mult,
         )
+        bias_gain = tail.tile([TOKENS, 1], F32)
+        nc.vector.tensor_scalar(
+            out=bias_gain[:], in0=link_sum[0:TOKENS, 1:2], scalar1=gain[:], scalar2=None, op0=ALU.mult
+        )
+        base = tail.tile([TOKENS, FEAT], F32)
+        nc.vector.scalar_tensor_tensor(
+            out=base[:],
+            in0=bf_all[0:TOKENS, 0:FEAT],
+            scalar=bias_gain[:],
+            in1=emb[:],
+            op0=ALU.mult,
+            op1=ALU.add,
+        )
         e = tail.tile([TOKENS, FEAT], F32)
         nc.vector.scalar_tensor_tensor(
-            out=e[:], in0=pooled[0:TOKENS, 0:FEAT], scalar=gain[:], in1=emb[:], op0=ALU.mult, op1=ALU.add
+            out=e[:], in0=pooled[0:TOKENS, 0:FEAT], scalar=gain[:], in1=base[:], op0=ALU.mult, op1=ALU.add
         )
         stats = tail.tile([TOKENS, 6], F32)
         nc.vector.bn_stats(out=stats[:], in_=e[:])

@@ -31,14 +31,14 @@ CHUNK_GROUPS = 4
 CHUNKS = GROUPS // CHUNK_GROUPS
 LAST_GROUPS = UNITS
 JOINT_GROUPS = GROUPS - LAST_GROUPS
-JOINT_CHUNKS = JOINT_GROUPS // CHUNK_GROUPS
 STEP_GROUPS = UNITS // ROW_TILES
 JOINT_STEPS = JOINT_GROUPS // STEP_GROUPS
 STEPS = JOINT_STEPS + ROW_TILES
-CHUNK_STEPS = CHUNK_GROUPS // STEP_GROUPS
-CHUNK_K = CHUNK_GROUPS * K_PASS
-X_BUFS = 4
-W_BUFS = 6
+X_LOADS = [1, 1, 1, 1, 2, 2, 4, 4, 4, 4]
+W_LOADS = [2, 2, 4, 4, 4, 4, 4, 4, 4]
+X_SMALL_BUFS = 6
+X_BUFS = 3
+W_BUFS = 5
 LN_EPS = 1e-5
 LINK_EPS = 1e-8
 
@@ -55,23 +55,22 @@ def tile_embed_update_pa_k_kernel(
     with ExitStack() as ctx:
         ctx.enter_context(tc.manual_schedule())
         consts = ctx.enter_context(tc.tile_pool(name="consts", bufs=1))
-        x_pool = ctx.enter_context(tc.tile_pool(name="x_pool", bufs=X_BUFS))
-        w_pool = ctx.enter_context(tc.tile_pool(name="w_pool", bufs=W_BUFS))
+        loads = ctx.enter_context(tc.tile_pool(name="loads", bufs=1))
         work = ctx.enter_context(tc.tile_pool(name="work", bufs=2))
         tail = ctx.enter_context(tc.tile_pool(name="tail", bufs=1))
         sums = ctx.enter_context(tc.psum_pool(name="sums", bufs=1))
         banks = ctx.enter_context(tc.psum_pool(name="banks", bufs=4))
 
         vecs = consts.tile([P, CH], BF16)
-        nc.vector.memset(vecs[:], 0.0)
-        w1_planes = consts.tile([P, CHUNKS, HID], U8, align_bytes=64)
+        nc.vector.memset(vecs[:].bitcast(I32), 0)
+        w1_planes = consts.tile([P, CHUNKS, HID], U8, align_bytes=256)
         nc.vector.memset(w1_planes[:, 0, :].bitcast(I32), 0)
         zero_col = consts.tile([P, 1], F32)
         nc.vector.memset(zero_col[:], 0.0)
         nc.vector.memset(w1_planes[:, 1:CHUNKS, :].bitcast(I32), 0)
         ident_f32 = consts.tile([P, P], F32)
         make_identity(nc, ident_f32[:])
-        wf_plane = consts.tile([P, CH], U8, align_bytes=64)
+        wf_plane = consts.tile([P, CH], U8, align_bytes=256)
         nc.gpsimd.memset(wf_plane[:].bitcast(I32), 0)
         token_of = consts.tile([P, P], F32)
         nc.gpsimd.memset(token_of[:], 0.0)
@@ -82,37 +81,39 @@ def tile_embed_update_pa_k_kernel(
         nc.scalar.dma_start(out=vecs[1:2, 0:CH], in_=b_f.rearrange("(o n) -> o n", o=1))
         nc.scalar.dma_start(out=vecs[2:3, 0:FEAT], in_=gamma.rearrange("(o n) -> o n", o=1))
         nc.scalar.dma_start(out=vecs[3:4, 0:FEAT], in_=beta.rearrange("(o n) -> o n", o=1))
-        m_bf = consts.tile([P, ROW_TILES], BF16)
-        nc.scalar.dma_start(
-            out=m_bf[:], in_=m.rearrange("b s k o -> (b s k o)").rearrange("(p r) -> p r", r=ROW_TILES)
-        )
-        emb = consts.tile([TOKENS, FEAT], BF16)
-        nc.scalar.dma_start(out=emb[:], in_=embeds.rearrange("b s c -> (b s) c"))
 
         warm = consts.tile([P, 1], F32)
         nc.scalar.activation(out=warm[:], in_=zero_col[:], func=ACT.Sigmoid)
 
-        x_tiles = {}
-        w_tiles = {}
+        x_place = {}
+        x_last = {}
+        w_place = {}
 
-        def load_x(c, pieces):
-            x_raw = x_pool.tile([P, ROW_TILES, CHUNK_K], BF16, name="x_raw")
-            first = 0
-            for groups in pieces:
-                last = first + groups * K_PASS
-                nc.sync.dma_start(
-                    out=x_raw[:, :, first:last],
-                    in_=x_dram[:, :, c * CHUNK_K + first : c * CHUNK_K + last],
-                )
-                first = last
-            x_tiles[c] = x_raw
+        def load_x(index):
+            first = sum(X_LOADS[:index])
+            groups = X_LOADS[index]
+            small = groups < CHUNK_GROUPS
+            x_raw = loads.tile(
+                [P, ROW_TILES, groups * K_PASS],
+                BF16,
+                name="x_raw",
+                tag="x_small" if small else "x_large",
+                bufs=X_SMALL_BUFS if small else X_BUFS,
+            )
+            nc.sync.dma_start(
+                out=x_raw[:], in_=x_dram[:, :, first * K_PASS : (first + groups) * K_PASS]
+            )
+            for g in range(groups):
+                x_place[first + g] = (x_raw, g)
 
         def load_x_last(r):
-            x_last = consts.tile([P, LAST_GROUPS * K_PASS], BF16, name="x_last%d" % r)
-            nc.sync.dma_start(out=x_last[:], in_=x_dram[:, r, JOINT_GROUPS * K_PASS : K_IN])
-            x_tiles[JOINT_CHUNKS + r] = x_last
+            x_raw = loads.tile(
+                [P, LAST_GROUPS * K_PASS], BF16, name="x_raw", tag="x_small", bufs=X_SMALL_BUFS
+            )
+            nc.sync.dma_start(out=x_raw[:], in_=x_dram[:, r, JOINT_GROUPS * K_PASS : K_IN])
+            x_last[r] = x_raw
 
-        def load_w(c):
+        def load_w_scales(c):
             for q in range(4):
                 nc.sync.dma_start(
                     out=w1_planes[32 * q : 32 * q + 16, c, :].bitcast(I32),
@@ -120,18 +121,42 @@ def tile_embed_update_pa_k_kernel(
                         c * CHUNK_GROUPS : (c + 1) * CHUNK_GROUPS, 4 * q : 4 * q + 4, :
                     ].bitcast(I32),
                 )
-            w_words = w_pool.tile([P, CHUNK_GROUPS, HID], U32, name="w_words", align_bytes=64)
-            nc.sync.dma_start(
-                out=w_words[:].bitcast(I32),
-                in_=w1_dram[:, c * CHUNK_GROUPS : (c + 1) * CHUNK_GROUPS, :],
-            )
-            w_tiles[c] = w_words
 
-        load_x(0, [1, 1, 2])
+        def load_w(index):
+            first = sum(W_LOADS[:index])
+            groups = W_LOADS[index]
+            small = groups < CHUNK_GROUPS
+            w_words = loads.tile(
+                [P, groups, HID],
+                U32,
+                name="w_words",
+                tag="w_small" if small else "w_large",
+                bufs=2 if small else W_BUFS,
+                align_bytes=256,
+            )
+            nc.sync.dma_start(out=w_words[:].bitcast(I32), in_=w1_dram[:, first : first + groups, :])
+            for g in range(groups):
+                w_place[first + g] = (w_words, g)
+
+        for index in range(4):
+            load_x(index)
+        load_w_scales(0)
         load_w(0)
-        for c in range(1, X_BUFS):
-            load_x(c, [CHUNK_GROUPS])
-            load_w(c)
+        load_w(1)
+        load_x(4)
+        load_x(5)
+        load_w_scales(1)
+        load_w(2)
+        for c in range(2, 2 + X_BUFS):
+            load_x(c + 4)
+            load_w_scales(c)
+            load_w(c + 1)
+        m_bf = consts.tile([P, ROW_TILES], BF16)
+        nc.sync.dma_start(
+            out=m_bf[:], in_=m.rearrange("b s k o -> (b s k o)").rearrange("(p r) -> p r", r=ROW_TILES)
+        )
+        emb = consts.tile([TOKENS, FEAT], BF16)
+        nc.sync.dma_start(out=emb[:], in_=embeds.rearrange("b s c -> (b s) c"))
 
         ident_bf = consts.tile([P, P], BF16)
         nc.vector.tensor_copy(out=ident_bf[:], in_=ident_f32[:])
@@ -168,10 +193,10 @@ def tile_embed_update_pa_k_kernel(
         def sort_step(i):
             x_sorted = work.tile([P, UNITS, 2, P], F32, name="x_sorted")
             if i < JOINT_STEPS:
-                c, h = divmod(i, CHUNK_STEPS)
-                words = x_tiles[c][:].bitcast(F32)
                 for g in range(STEP_GROUPS):
-                    first = (h * STEP_GROUPS + g) * PAIR_WORDS
+                    x_raw, place = x_place[STEP_GROUPS * i + g]
+                    words = x_raw[:].bitcast(F32)
+                    first = place * PAIR_WORDS
                     nc.vector.tensor_copy(
                         out=x_sorted[:, g * ROW_TILES : (g + 1) * ROW_TILES, :, :],
                         in_=words[:, :, first : first + PAIR_WORDS].rearrange(
@@ -179,7 +204,7 @@ def tile_embed_update_pa_k_kernel(
                         ),
                     )
             else:
-                words = x_tiles[JOINT_CHUNKS + i - JOINT_STEPS][:].bitcast(F32)
+                words = x_last[i - JOINT_STEPS][:].bitcast(F32)
                 nc.vector.tensor_copy(
                     out=x_sorted[:], in_=words.rearrange("p (k q u) -> p k u q", u=2, q=P)
                 )
@@ -187,7 +212,7 @@ def tile_embed_update_pa_k_kernel(
 
         def transpose_step(i):
             x_sorted = sorted_tiles[i]
-            grouped = work.tile([P, UNITS, K_PASS], BF16, name="grouped", align_bytes=64)
+            grouped = work.tile([P, UNITS, K_PASS], BF16, name="grouped", align_bytes=256)
             grouped_words = grouped[:].bitcast(F32)
             for k in range(0, UNITS, 2):
                 bank = banks.tile([P, 4 * P], F32, name="bank")
@@ -208,8 +233,8 @@ def tile_embed_update_pa_k_kernel(
 
         def quantise_step(i, part):
             if part == 0:
-                x_codes = work.tile([P, UNITS, P], U32, name="x_codes", align_bytes=64)
-                x_planes = work.tile([P, UNITS, P], U8, name="x_planes", align_bytes=64)
+                x_codes = work.tile([P, UNITS, P], U32, name="x_codes", align_bytes=256)
+                x_planes = work.tile([P, UNITS, P], U8, name="x_planes", align_bytes=256)
                 code_tiles[i] = (x_codes, x_planes)
             x_codes, x_planes = code_tiles[i]
             units = slice(part * CALL_UNITS, (part + 1) * CALL_UNITS)
@@ -221,26 +246,29 @@ def tile_embed_update_pa_k_kernel(
 
         def multiply_step(i):
             x_codes, x_planes = code_tiles[i]
-            for k, (r, group) in enumerate(units_of(i)):
+            units = units_of(i)
+            for k in sorted(range(UNITS), key=lambda k: units[k]):
+                r, group = units[k]
                 c, j = divmod(group, CHUNK_GROUPS)
+                w_words, place = w_place[group]
                 nc.tensor.matmul_mx(
                     out=acc[r][:],
                     lhsT=x_codes[:, k, :].bitcast(FP8X4),
                     lhsT_scale=x_planes[:, k, :],
-                    rhs=w_tiles[c][:, j, :].bitcast(FP8X4),
+                    rhs=w_words[:, place, :].bitcast(FP8X4),
                     rhs_scale=w1_planes[4 * j : P, c, :],
                     start=(group == 0),
                     stop=(group == GROUPS - 1),
                 )
 
-        wf_words = consts.tile([P, CH], U32, align_bytes=64)
+        wf_words = consts.tile([P, CH], U32, align_bytes=256)
         pre_h = tail.tile([P, ROW_TILES, HID], BF16)
         h_grouped = tail.tile([P, ROW_TILES, HID], BF16, align_bytes=64)
         h_codes = tail.tile([P, ROW_TILES, P], U32, align_bytes=64)
         h_planes = tail.tile([P, ROW_TILES, P], U8, align_bytes=64)
         gate = tail.tile([P, ROW_TILES], F32)
         link_cols = tail.tile([P, ROW_TILES, 3], F32)
-        weighted = tail.tile([P, ROW_TILES, FEAT], F32)
+        weighted = {}
         m_f32 = consts.tile([P, ROW_TILES], F32)
         m_sq = consts.tile([P, ROW_TILES], F32)
         m_eps = consts.tile([P, ROW_TILES], F32)
@@ -288,6 +316,7 @@ def tile_embed_update_pa_k_kernel(
 
         def weigh_links(r):
             s = gate[:, r : r + 1]
+            weighted[r] = tail.tile([P, FEAT], F32, name="weighted", bufs=2)
             nc.vector.tensor_scalar(
                 out=link_cols[:, r, 1:2],
                 in0=s,
@@ -298,7 +327,7 @@ def tile_embed_update_pa_k_kernel(
             )
             if r == 0:
                 nc.vector.tensor_scalar(
-                    out=weighted[:, r, :],
+                    out=weighted[r][:],
                     in0=o_sum[r][:, 0:FEAT],
                     scalar1=link_cols[:, r, 1:2],
                     scalar2=None,
@@ -306,10 +335,10 @@ def tile_embed_update_pa_k_kernel(
                 )
             else:
                 nc.vector.scalar_tensor_tensor(
-                    out=weighted[:, r, :],
+                    out=weighted[r][:],
                     in0=o_sum[r][:, 0:FEAT],
                     scalar=link_cols[:, r, 1:2],
-                    in1=weighted[:, r - 1, :],
+                    in1=weighted[r - 1][:],
                     op0=ALU.mult,
                     op1=ALU.add,
                 )
@@ -344,21 +373,21 @@ def tile_embed_update_pa_k_kernel(
             if i + 1 < STEPS:
                 sort_step(i + 1)
 
-            if i == 0:
-                load_x(X_BUFS, [CHUNK_GROUPS])
-                load_w(X_BUFS)
-            if i == 2:
-                load_x(X_BUFS + 1, [CHUNK_GROUPS])
-                load_w(X_BUFS + 1)
+            if i == 8:
                 nc.vector.tensor_copy(out=m_f32[:], in_=m_bf[:])
                 nc.vector.tensor_tensor(out=m_sq[:], in0=m_f32[:], in1=m_f32[:], op=ALU.mult)
                 nc.vector.tensor_scalar(
                     out=m_eps[:], in0=m_f32[:], scalar1=LINK_EPS, scalar2=None, op0=ALU.mult
                 )
             if i == 4:
+                load_x(9)
+                load_w_scales(5)
+                load_w(6)
+            if i == 6:
                 load_x_last(0)
-                load_w(JOINT_CHUNKS)
-                load_w(JOINT_CHUNKS + 1)
+                for c in (6, 7):
+                    load_w_scales(c)
+                    load_w(c + 1)
                 for q in range(4):
                     nc.sync.dma_start(
                         out=wf_plane[32 * q : 32 * q + 4, :].bitcast(I32),
@@ -400,7 +429,7 @@ def tile_embed_update_pa_k_kernel(
             )
         pooled = banks.tile([P, 4 * P], F32, name="bank")
         nc.tensor.matmul(
-            out=pooled[:, 0:FEAT], lhsT=token_of[:], rhs=weighted[:, ROW_TILES - 1, :], start=True, stop=True
+            out=pooled[:, 0:FEAT], lhsT=token_of[:], rhs=weighted[ROW_TILES - 1][:], start=True, stop=True
         )
 
         inv = tail.tile([TOKENS, 1], F32)

@@ -29,16 +29,13 @@ UNITS = 8
 CALL_UNITS = 4
 CHUNK_GROUPS = 4
 CHUNKS = GROUPS // CHUNK_GROUPS
-LAST_GROUPS = UNITS
-JOINT_GROUPS = GROUPS - LAST_GROUPS
-STEP_GROUPS = UNITS // ROW_TILES
-JOINT_STEPS = JOINT_GROUPS // STEP_GROUPS
-STEPS = JOINT_STEPS + ROW_TILES
-X_LOADS = [1, 1, 1, 1, 2, 2, 4, 4, 4, 4]
-W_LOADS = [2, 2, 4, 4, 4, 4, 4, 4, 4]
-X_SMALL_BUFS = 6
-X_BUFS = 3
+CHUNK_K = CHUNK_GROUPS * K_PASS
+STEP_TILES = UNITS // CHUNK_GROUPS
+CHUNK_STEPS = ROW_TILES // STEP_TILES
+STEPS = CHUNKS * CHUNK_STEPS
+X_BUFS = 10
 W_BUFS = 5
+HALF = 256
 LN_EPS = 1e-5
 LINK_EPS = 1e-8
 
@@ -86,34 +83,18 @@ def tile_embed_update_pa_k_kernel(
         nc.scalar.activation(out=warm[:], in_=zero_col[:], func=ACT.Sigmoid)
 
         x_place = {}
-        x_last = {}
         w_place = {}
 
-        def load_x(index):
-            first = sum(X_LOADS[:index])
-            groups = X_LOADS[index]
-            small = groups < CHUNK_GROUPS
-            x_raw = loads.tile(
-                [P, ROW_TILES, groups * K_PASS],
-                BF16,
-                name="x_raw",
-                tag="x_small" if small else "x_large",
-                bufs=X_SMALL_BUFS if small else X_BUFS,
-            )
+        def load_x(c, tiles):
+            x_raw = loads.tile([P, len(tiles), CHUNK_K], BF16, name="x_raw", bufs=X_BUFS)
             nc.sync.dma_start(
-                out=x_raw[:], in_=x_dram[:, :, first * K_PASS : (first + groups) * K_PASS]
+                out=x_raw[:],
+                in_=x_dram[:, tiles[0] : tiles[-1] + 1, c * CHUNK_K : (c + 1) * CHUNK_K],
             )
-            for g in range(groups):
-                x_place[first + g] = (x_raw, g)
+            for place, r in enumerate(tiles):
+                x_place[r, c] = x_raw[:, place, :]
 
-        def load_x_last(r):
-            x_raw = loads.tile(
-                [P, LAST_GROUPS * K_PASS], BF16, name="x_raw", tag="x_small", bufs=X_SMALL_BUFS
-            )
-            nc.sync.dma_start(out=x_raw[:], in_=x_dram[:, r, JOINT_GROUPS * K_PASS : K_IN])
-            x_last[r] = x_raw
-
-        def load_w_scales(c):
+        def load_scales(c):
             for q in range(4):
                 nc.sync.dma_start(
                     out=w1_planes[32 * q : 32 * q + 16, c, :].bitcast(I32),
@@ -122,35 +103,33 @@ def tile_embed_update_pa_k_kernel(
                     ].bitcast(I32),
                 )
 
-        def load_w(index):
-            first = sum(W_LOADS[:index])
-            groups = W_LOADS[index]
-            small = groups < CHUNK_GROUPS
+        def load_w(first, groups):
+            whole = groups == CHUNK_GROUPS
             w_words = loads.tile(
                 [P, groups, HID],
                 U32,
                 name="w_words",
-                tag="w_small" if small else "w_large",
-                bufs=2 if small else W_BUFS,
+                tag="w_chunk" if whole else "w_part",
+                bufs=W_BUFS if whole else 2,
                 align_bytes=256,
             )
             nc.sync.dma_start(out=w_words[:].bitcast(I32), in_=w1_dram[:, first : first + groups, :])
             for g in range(groups):
-                w_place[first + g] = (w_words, g)
+                w_place[first + g] = w_words[:, g, :]
 
-        for index in range(4):
-            load_x(index)
-        load_w_scales(0)
-        load_w(0)
-        load_w(1)
-        load_x(4)
-        load_x(5)
-        load_w_scales(1)
-        load_w(2)
-        for c in range(2, 2 + X_BUFS):
-            load_x(c + 4)
-            load_w_scales(c)
-            load_w(c + 1)
+        def load_chunk(c):
+            for s in range(CHUNK_STEPS):
+                load_x(c, list(range(s * STEP_TILES, (s + 1) * STEP_TILES)))
+            load_scales(c)
+            load_w(c * CHUNK_GROUPS, CHUNK_GROUPS)
+
+        for r in range(ROW_TILES):
+            load_x(0, [r])
+        load_scales(0)
+        load_w(0, CHUNK_GROUPS // 2)
+        load_w(CHUNK_GROUPS // 2, CHUNK_GROUPS // 2)
+        for c in range(1, 4):
+            load_chunk(c)
         m_bf = consts.tile([P, ROW_TILES], BF16)
         nc.sync.dma_start(
             out=m_bf[:], in_=m.rearrange("b s k o -> (b s k o)").rearrange("(p r) -> p r", r=ROW_TILES)
@@ -186,27 +165,22 @@ def tile_embed_update_pa_k_kernel(
         grouped_tiles = {}
 
         def units_of(i):
-            if i < JOINT_STEPS:
-                return [(r, STEP_GROUPS * i + g) for g in range(STEP_GROUPS) for r in range(ROW_TILES)]
-            return [(i - JOINT_STEPS, JOINT_GROUPS + g) for g in range(LAST_GROUPS)]
+            c, s = divmod(i, CHUNK_STEPS)
+            return [
+                (s * STEP_TILES + r, c * CHUNK_GROUPS + g)
+                for r in range(STEP_TILES)
+                for g in range(CHUNK_GROUPS)
+            ]
 
         def sort_step(i):
             x_sorted = work.tile([P, UNITS, 2, P], F32, name="x_sorted")
-            if i < JOINT_STEPS:
-                for g in range(STEP_GROUPS):
-                    x_raw, place = x_place[STEP_GROUPS * i + g]
-                    words = x_raw[:].bitcast(F32)
-                    first = place * PAIR_WORDS
-                    nc.vector.tensor_copy(
-                        out=x_sorted[:, g * ROW_TILES : (g + 1) * ROW_TILES, :, :],
-                        in_=words[:, :, first : first + PAIR_WORDS].rearrange(
-                            "p r (q u) -> p r u q", u=2
-                        ),
-                    )
-            else:
-                words = x_last[i - JOINT_STEPS][:].bitcast(F32)
+            c, s = divmod(i, CHUNK_STEPS)
+            for r in range(STEP_TILES):
                 nc.vector.tensor_copy(
-                    out=x_sorted[:], in_=words.rearrange("p (k q u) -> p k u q", u=2, q=P)
+                    out=x_sorted[:, r * CHUNK_GROUPS : (r + 1) * CHUNK_GROUPS, :, :],
+                    in_=x_place[s * STEP_TILES + r, c]
+                    .bitcast(F32)
+                    .rearrange("p (g q u) -> p g u q", u=2, q=P),
                 )
             sorted_tiles[i] = x_sorted
 
@@ -246,16 +220,13 @@ def tile_embed_update_pa_k_kernel(
 
         def multiply_step(i):
             x_codes, x_planes = code_tiles[i]
-            units = units_of(i)
-            for k in sorted(range(UNITS), key=lambda k: units[k]):
-                r, group = units[k]
+            for k, (r, group) in enumerate(units_of(i)):
                 c, j = divmod(group, CHUNK_GROUPS)
-                w_words, place = w_place[group]
                 nc.tensor.matmul_mx(
                     out=acc[r][:],
                     lhsT=x_codes[:, k, :].bitcast(FP8X4),
                     lhsT_scale=x_planes[:, k, :],
-                    rhs=w_words[:, place, :].bitcast(FP8X4),
+                    rhs=w_place[group].bitcast(FP8X4),
                     rhs_scale=w1_planes[4 * j : P, c, :],
                     start=(group == 0),
                     stop=(group == GROUPS - 1),
@@ -267,8 +238,9 @@ def tile_embed_update_pa_k_kernel(
         h_codes = tail.tile([P, ROW_TILES, P], U32, align_bytes=64)
         h_planes = tail.tile([P, ROW_TILES, P], U8, align_bytes=64)
         gate = tail.tile([P, ROW_TILES], F32)
-        link_cols = tail.tile([P, ROW_TILES, 3], F32)
-        weighted = {}
+        link_l = tail.tile([P, ROW_TILES], F32)
+        link_lm = tail.tile([P, ROW_TILES], F32)
+        link_lms = tail.tile([P, ROW_TILES], F32)
         m_f32 = consts.tile([P, ROW_TILES], F32)
         m_sq = consts.tile([P, ROW_TILES], F32)
         m_eps = consts.tile([P, ROW_TILES], F32)
@@ -277,6 +249,8 @@ def tile_embed_update_pa_k_kernel(
         def add_bias(r):
             nc.vector.tensor_tensor(out=pre_h[:, r, :], in0=acc[r][:], in1=b1_all[:], op=ALU.add)
 
+        hidden_banks = {}
+
         def transpose_hidden(r):
             pre_h_words = pre_h[:].bitcast(F32)
             bank = banks.tile([P, 4 * P], F32, name="bank")
@@ -284,11 +258,15 @@ def tile_embed_update_pa_k_kernel(
                 nc.tensor.transpose(
                     bank[:, u * P : (u + 1) * P], pre_h_words[:, r, u : PAIR_WORDS : 2], ident_f32[:]
                 )
-            nc.scalar.activation(
-                out=h_grouped[:, r, :].rearrange("p (j u e) -> p j u e", u=2, e=2),
-                in_=bank[:, 0 : 2 * P].bitcast(BF16).rearrange("p (u j e) -> p j u e", u=2, e=2),
-                func=ACT.Relu,
-            )
+            hidden_banks[r] = bank
+
+        def relu_hidden(r):
+            h_out = h_grouped[:, r, :].rearrange("p (j u e) -> p j u e", u=2, e=2)
+            h_in = hidden_banks[r][:, 0 : 2 * P].bitcast(BF16).rearrange("p (u j e) -> p j u e", u=2, e=2)
+            if r % 2 == 0:
+                nc.scalar.activation(out=h_out, in_=h_in, func=ACT.Relu)
+            else:
+                nc.vector.tensor_scalar(out=h_out, in0=h_in, scalar1=0.0, scalar2=None, op0=ALU.max)
 
         def quantise_hidden(r):
             nc.vector.quantize_mx(
@@ -306,88 +284,75 @@ def tile_embed_update_pa_k_kernel(
                 start=True,
                 stop=True,
             )
+            o_sum[r] = o_ps
+
+        def score_links(r):
             nc.scalar.activation(
                 out=gate[:, r : r + 1],
-                in_=o_ps[:, FEAT:CH],
+                in_=o_sum[r][:, FEAT:CH],
                 func=ACT.Sigmoid,
                 bias=bf_all[:, FEAT:CH],
             )
-            o_sum[r] = o_ps
-
-        def weigh_links(r):
-            s = gate[:, r : r + 1]
-            weighted[r] = tail.tile([P, FEAT], F32, name="weighted", bufs=2)
             nc.vector.tensor_scalar(
-                out=link_cols[:, r, 1:2],
-                in0=s,
+                out=link_lm[:, r : r + 1],
+                in0=gate[:, r : r + 1],
                 scalar1=m_sq[:, r : r + 1],
                 scalar2=m_eps[:, r : r + 1],
                 op0=ALU.mult,
                 op1=ALU.add,
             )
-            if r == 0:
-                nc.vector.tensor_scalar(
-                    out=weighted[r][:],
-                    in0=o_sum[r][:, 0:FEAT],
-                    scalar1=link_cols[:, r, 1:2],
-                    scalar2=None,
-                    op0=ALU.mult,
-                )
-            else:
-                nc.vector.scalar_tensor_tensor(
-                    out=weighted[r][:],
-                    in0=o_sum[r][:, 0:FEAT],
-                    scalar=link_cols[:, r, 1:2],
-                    in1=weighted[r - 1][:],
-                    op0=ALU.mult,
-                    op1=ALU.add,
-                )
-            nc.vector.tensor_scalar(
-                out=link_cols[:, r, 0:1],
-                in0=s,
-                scalar1=m_f32[:, r : r + 1],
-                scalar2=LINK_EPS,
+
+        weighted = {}
+
+        def weigh_even(r):
+            part = tail.tile([P, FEAT], F32, name="even%d" % r)
+            nc.scalar.activation(
+                out=part[:], in_=o_sum[r][:, 0:FEAT], func=ACT.Copy, scale=link_lm[:, r : r + 1]
+            )
+            weighted[r] = part
+
+        def weigh_odd(r, first, last):
+            if first == 0:
+                weighted[r] = tail.tile([P, FEAT], F32, name="odd%d" % r)
+            nc.vector.scalar_tensor_tensor(
+                out=weighted[r][:, first:last],
+                in0=o_sum[r][:, first:last],
+                scalar=link_lm[:, r : r + 1],
+                in1=weighted[r - 1][:, first:last],
                 op0=ALU.mult,
                 op1=ALU.add,
             )
-            nc.vector.tensor_tensor(
-                out=link_cols[:, r, 2:3], in0=link_cols[:, r, 1:2], in1=s, op=ALU.mult
-            )
+
+        def multiply(i):
+            quantise_step(i, 0)
+            quantise_step(i, 1)
+            multiply_step(i)
 
         sort_step(0)
-        for i in range(STEPS):
-            done = i - 2 - JOINT_STEPS
+        transpose_step(0)
+        sort_step(1)
+        transpose_step(1)
+        load_chunk(4)
+        load_chunk(5)
+        multiply(0)
+        multiply(1)
+        sort_step(2)
+        transpose_step(2)
+        sort_step(3)
+        for i in range(3, STEPS):
             transpose_step(i)
-            if i >= 1:
-                quantise_step(i - 1, 0)
-                if done >= 1:
-                    quantise_hidden(done - 1)
-                quantise_step(i - 1, 1)
-            if done >= 0:
-                add_bias(done)
-                transpose_hidden(done)
-            if i >= 1:
-                multiply_step(i - 1)
-            if done >= 1:
-                multiply_hidden(done - 1)
+            multiply(i - 1)
             if i + 1 < STEPS:
                 sort_step(i + 1)
-
+            if i == 4:
+                load_chunk(6)
             if i == 8:
                 nc.vector.tensor_copy(out=m_f32[:], in_=m_bf[:])
                 nc.vector.tensor_tensor(out=m_sq[:], in0=m_f32[:], in1=m_f32[:], op=ALU.mult)
                 nc.vector.tensor_scalar(
                     out=m_eps[:], in0=m_f32[:], scalar1=LINK_EPS, scalar2=None, op0=ALU.mult
                 )
-            if i == 4:
-                load_x(9)
-                load_w_scales(5)
-                load_w(6)
             if i == 6:
-                load_x_last(0)
-                for c in (6, 7):
-                    load_w_scales(c)
-                    load_w(c + 1)
                 for q in range(4):
                     nc.sync.dma_start(
                         out=wf_plane[32 * q : 32 * q + 4, :].bitcast(I32),
@@ -397,55 +362,78 @@ def tile_embed_update_pa_k_kernel(
                     out=wf_words[:].bitcast(I32),
                     in_=Wf_words[0].rearrange("p n t -> p (n t)").bitcast(I32),
                 )
-                for r in range(1, ROW_TILES):
-                    load_x_last(r)
+                load_chunk(7)
+        multiply(STEPS - 1)
 
-        quantise_step(STEPS - 1, 0)
-        quantise_hidden(1)
-        quantise_step(STEPS - 1, 1)
-        multiply_hidden(1)
-        add_bias(2)
-        weigh_links(0)
-        weigh_links(1)
-        multiply_step(STEPS - 1)
-        transpose_hidden(2)
-        add_bias(3)
-        transpose_hidden(3)
-        quantise_hidden(2)
-        multiply_hidden(2)
-        quantise_hidden(3)
-        multiply_hidden(3)
-        weigh_links(2)
-        weigh_links(3)
-
-        link_sum = banks.tile([P, 4 * P], F32, name="bank")
         for r in range(ROW_TILES):
+            add_bias(r)
+            transpose_hidden(r)
+        relu_hidden(0)
+        relu_hidden(1)
+        relu_hidden(2)
+        quantise_hidden(0)
+        multiply_hidden(0)
+        relu_hidden(3)
+        for r in range(1, ROW_TILES):
+            quantise_hidden(r)
+            multiply_hidden(r)
+
+        pooled = [banks.tile([P, 4 * P], F32, name="bank") for j in range(2)]
+        halves = [(0, HALF), (HALF, FEAT)]
+
+        def pool_half(r, j):
+            first, last = halves[j]
             nc.tensor.matmul(
-                out=link_sum[:, 0:3],
+                out=pooled[j][:, 0 : last - first],
                 lhsT=token_of[:],
-                rhs=link_cols[:, r, :],
-                start=(r == 0),
+                rhs=weighted[r][:, first:last],
+                start=(r == 1),
                 stop=(r == ROW_TILES - 1),
             )
-        pooled = banks.tile([P, 4 * P], F32, name="bank")
-        nc.tensor.matmul(
-            out=pooled[:, 0:FEAT], lhsT=token_of[:], rhs=weighted[ROW_TILES - 1][:], start=True, stop=True
-        )
 
+        score_links(0)
+        score_links(1)
+        weigh_even(0)
+        weigh_odd(1, 0, FEAT)
+        pool_half(1, 0)
+        pool_half(1, 1)
+        score_links(2)
+        score_links(3)
+        weigh_even(2)
+        nc.gpsimd.tensor_tensor(out=link_l[:], in0=gate[:], in1=m_f32[:], op=ALU.mult)
+        nc.gpsimd.tensor_tensor(out=link_lms[:], in0=link_lm[:], in1=gate[:], op=ALU.mult)
+        nc.gpsimd.tensor_scalar(
+            out=link_l[:], in0=link_l[:], scalar1=1.0, scalar2=LINK_EPS, op0=ALU.mult, op1=ALU.add
+        )
+        link_sum = banks.tile([P, 4 * P], F32, name="bank")
+        for j, cols in enumerate((link_l, link_lm, link_lms)):
+            nc.tensor.matmul(
+                out=link_sum[:, j * ROW_TILES : (j + 1) * ROW_TILES],
+                lhsT=token_of[:],
+                rhs=cols[:],
+                start=True,
+                stop=True,
+            )
+        for j in range(2):
+            weigh_odd(3, halves[j][0], halves[j][1])
+            pool_half(3, j)
+
+        total = tail.tile([TOKENS, 3], F32)
+        nc.vector.tensor_reduce(
+            out=total[:],
+            in_=link_sum[0:TOKENS, 0 : 3 * ROW_TILES].rearrange("p (j r) -> p j r", r=ROW_TILES),
+            axis=AXIS.X,
+            op=ALU.add,
+        )
         inv = tail.tile([TOKENS, 1], F32)
-        nc.vector.reciprocal(out=inv[:], in_=link_sum[0:TOKENS, 0:1])
+        nc.vector.reciprocal(out=inv[:], in_=total[:, 0:1])
         gain = tail.tile([TOKENS, 1], F32)
         nc.vector.tensor_scalar(
-            out=gain[:],
-            in0=link_sum[0:TOKENS, 2:3],
-            scalar1=inv[:],
-            scalar2=inv[:],
-            op0=ALU.mult,
-            op1=ALU.mult,
+            out=gain[:], in0=total[:, 2:3], scalar1=inv[:], scalar2=inv[:], op0=ALU.mult, op1=ALU.mult
         )
         bias_gain = tail.tile([TOKENS, 1], F32)
         nc.vector.tensor_scalar(
-            out=bias_gain[:], in0=link_sum[0:TOKENS, 1:2], scalar1=gain[:], scalar2=None, op0=ALU.mult
+            out=bias_gain[:], in0=total[:, 1:2], scalar1=gain[:], scalar2=None, op0=ALU.mult
         )
         base = tail.tile([TOKENS, FEAT], F32)
         nc.vector.scalar_tensor_tensor(
@@ -457,13 +445,20 @@ def tile_embed_update_pa_k_kernel(
             op1=ALU.add,
         )
         e = tail.tile([TOKENS, FEAT], F32)
-        nc.vector.scalar_tensor_tensor(
-            out=e[:], in0=pooled[0:TOKENS, 0:FEAT], scalar=gain[:], in1=base[:], op0=ALU.mult, op1=ALU.add
-        )
-        stats = tail.tile([TOKENS, 6], F32)
-        nc.vector.bn_stats(out=stats[:], in_=e[:])
+        stats = tail.tile([TOKENS, 2, 6], F32)
+        for j, (first, last) in enumerate(halves):
+            nc.vector.scalar_tensor_tensor(
+                out=e[:, first:last],
+                in0=pooled[j][0:TOKENS, 0 : last - first],
+                scalar=gain[:],
+                in1=base[:, first:last],
+                op0=ALU.mult,
+                op1=ALU.add,
+            )
+        for j, (first, last) in enumerate(halves):
+            nc.vector.bn_stats(out=stats[:, j, :], in_=e[:, first:last])
         mean_var = tail.tile([TOKENS, 2], F32)
-        nc.vector.bn_aggr(out=mean_var[:], in_=stats[:])
+        nc.vector.bn_aggr(out=mean_var[:], in_=stats[:].rearrange("p j s -> p (j s)"))
         var_eps = tail.tile([TOKENS, 1], F32)
         nc.vector.tensor_scalar_add(out=var_eps[:], in0=mean_var[:, 1:2], scalar1=LN_EPS)
         rstd = tail.tile([TOKENS, 1], F32)

@@ -67,12 +67,14 @@ def tile_embed_update_pa_k_kernel(
         nc.vector.memset(w1_planes[:, 1:CHUNKS, :].bitcast(I32), 0)
         ident_f32 = consts.tile([P, P], F32)
         make_identity(nc, ident_f32[:])
+        eps_col = consts.tile([P, 1], F32)
+        nc.vector.tensor_scalar(
+            out=eps_col[:], in0=zero_col[:], scalar1=1.0, scalar2=LN_EPS, op0=ALU.mult, op1=ALU.add
+        )
         wf_plane = consts.tile([P, CH], U8, align_bytes=256)
         nc.gpsimd.memset(wf_plane[:].bitcast(I32), 0)
         token_of = consts.tile([P, P], F32)
         nc.gpsimd.memset(token_of[:], 0.0)
-        neg_half = consts.tile([TOKENS, 1], F32)
-        nc.gpsimd.memset(neg_half[:], -0.5)
 
         nc.scalar.dma_start(out=vecs[0:1, 0:HID], in_=b1.rearrange("(o n) -> o n", o=1))
         nc.scalar.dma_start(out=vecs[1:2, 0:CH], in_=b_f.rearrange("(o n) -> o n", o=1))
@@ -263,7 +265,7 @@ def tile_embed_update_pa_k_kernel(
         def relu_hidden(r):
             h_out = h_grouped[:, r, :].rearrange("p (j u e) -> p j u e", u=2, e=2)
             h_in = hidden_banks[r][:, 0 : 2 * P].bitcast(BF16).rearrange("p (u j e) -> p j u e", u=2, e=2)
-            if r % 2 == 0:
+            if r < ROW_TILES - 1:
                 nc.scalar.activation(out=h_out, in_=h_in, func=ACT.Relu)
             else:
                 nc.vector.tensor_scalar(out=h_out, in0=h_in, scalar1=0.0, scalar2=None, op0=ALU.max)
@@ -293,6 +295,8 @@ def tile_embed_update_pa_k_kernel(
                 func=ACT.Sigmoid,
                 bias=bf_all[:, FEAT:CH],
             )
+
+        def link_weight(r):
             nc.vector.tensor_scalar(
                 out=link_lm[:, r : r + 1],
                 in0=gate[:, r : r + 1],
@@ -304,24 +308,21 @@ def tile_embed_update_pa_k_kernel(
 
         weighted = {}
 
-        def weigh_even(r):
-            part = tail.tile([P, FEAT], F32, name="even%d" % r)
-            nc.scalar.activation(
-                out=part[:], in_=o_sum[r][:, 0:FEAT], func=ACT.Copy, scale=link_lm[:, r : r + 1]
-            )
-            weighted[r] = part
-
-        def weigh_odd(r, first, last):
+        def weigh(r, onto, first, last):
             if first == 0:
-                weighted[r] = tail.tile([P, FEAT], F32, name="odd%d" % r)
+                weighted[r] = tail.tile([P, FEAT], F32, name="weighted%d" % r)
             nc.vector.scalar_tensor_tensor(
                 out=weighted[r][:, first:last],
                 in0=o_sum[r][:, first:last],
                 scalar=link_lm[:, r : r + 1],
-                in1=weighted[r - 1][:, first:last],
+                in1=weighted[onto][:, first:last],
                 op0=ALU.mult,
                 op1=ALU.add,
             )
+
+        def keep_warm(idle, count):
+            for j in range(count):
+                nc.tensor.matmul(out=idle[:], lhsT=ident_bf[:], rhs=vecs[:], start=True, stop=True)
 
         def multiply(i):
             quantise_step(i, 0)
@@ -368,15 +369,20 @@ def tile_embed_update_pa_k_kernel(
         for r in range(ROW_TILES):
             add_bias(r)
             transpose_hidden(r)
+        keep_warm(sums.tile([P, CH], F32, name="idle0", tag="sum0"), 1)
         relu_hidden(0)
         relu_hidden(1)
         relu_hidden(2)
         quantise_hidden(0)
         multiply_hidden(0)
+        score_links(0)
+        keep_warm(sums.tile([P, CH], F32, name="idle1", tag="sum1"), 1)
         relu_hidden(3)
-        for r in range(1, ROW_TILES):
+        for r in (1, 3, 2):
             quantise_hidden(r)
             multiply_hidden(r)
+            score_links(r)
+        keep_warm(banks.tile([P, CH], F32, name="bank"), 3)
 
         pooled = [banks.tile([P, 4 * P], F32, name="bank") for j in range(2)]
         halves = [(0, HALF), (HALF, FEAT)]
@@ -387,24 +393,35 @@ def tile_embed_update_pa_k_kernel(
                 out=pooled[j][:, 0 : last - first],
                 lhsT=token_of[:],
                 rhs=weighted[r][:, first:last],
-                start=(r == 1),
-                stop=(r == ROW_TILES - 1),
+                start=(r == ROW_TILES - 1),
+                stop=(r != ROW_TILES - 1),
             )
 
-        score_links(0)
-        score_links(1)
-        weigh_even(0)
-        weigh_odd(1, 0, FEAT)
-        pool_half(1, 0)
-        pool_half(1, 1)
-        score_links(2)
-        score_links(3)
-        weigh_even(2)
+        link_weight(0)
+        weighted[0] = tail.tile([P, FEAT], F32, name="weighted0")
+        nc.vector.tensor_scalar(
+            out=weighted[0][:],
+            in0=o_sum[0][:, 0:FEAT],
+            scalar1=link_lm[:, 0:1],
+            scalar2=None,
+            op0=ALU.mult,
+        )
+        link_weight(1)
+        link_weight(3)
+        weighted[3] = tail.tile([P, FEAT], F32, name="weighted3")
+        nc.scalar.activation(
+            out=weighted[3][:], in_=o_sum[3][:, 0:FEAT], func=ACT.Copy, scale=link_lm[:, 3:4]
+        )
+        weigh(1, 0, 0, FEAT)
+        link_weight(2)
+        nc.scalar.activation(out=warm[:], in_=eps_col[:], func=ACT.Abs_reciprocal_sqrt)
         nc.gpsimd.tensor_tensor(out=link_l[:], in0=gate[:], in1=m_f32[:], op=ALU.mult)
         nc.gpsimd.tensor_tensor(out=link_lms[:], in0=link_lm[:], in1=gate[:], op=ALU.mult)
         nc.gpsimd.tensor_scalar(
             out=link_l[:], in0=link_l[:], scalar1=1.0, scalar2=LINK_EPS, op0=ALU.mult, op1=ALU.add
         )
+        for j in range(2):
+            pool_half(3, j)
         link_sum = banks.tile([P, 4 * P], F32, name="bank")
         for j, cols in enumerate((link_l, link_lm, link_lms)):
             nc.tensor.matmul(
@@ -415,8 +432,8 @@ def tile_embed_update_pa_k_kernel(
                 stop=True,
             )
         for j in range(2):
-            weigh_odd(3, halves[j][0], halves[j][1])
-            pool_half(3, j)
+            weigh(2, 1, halves[j][0], halves[j][1])
+            pool_half(2, j)
 
         total = tail.tile([TOKENS, 3], F32)
         nc.vector.tensor_reduce(
@@ -459,10 +476,13 @@ def tile_embed_update_pa_k_kernel(
             nc.vector.bn_stats(out=stats[:, j, :], in_=e[:, first:last])
         mean_var = tail.tile([TOKENS, 2], F32)
         nc.vector.bn_aggr(out=mean_var[:], in_=stats[:].rearrange("p j s -> p (j s)"))
-        var_eps = tail.tile([TOKENS, 1], F32)
-        nc.vector.tensor_scalar_add(out=var_eps[:], in0=mean_var[:, 1:2], scalar1=LN_EPS)
         rstd = tail.tile([TOKENS, 1], F32)
-        nc.gpsimd.tensor_tensor(out=rstd[:], in0=var_eps[:], in1=neg_half[:], op=ALU.pow)
+        nc.scalar.activation(
+            out=rstd[:],
+            in_=mean_var[:, 1:2],
+            func=ACT.Abs_reciprocal_sqrt,
+            bias=eps_col[0:TOKENS, :],
+        )
         centred = tail.tile([TOKENS, FEAT], F32)
         nc.vector.scalar_tensor_tensor(
             out=centred[:],

@@ -30,9 +30,8 @@ CALL_UNITS = 4
 CHUNK_GROUPS = 4
 CHUNKS = GROUPS // CHUNK_GROUPS
 CHUNK_K = CHUNK_GROUPS * K_PASS
-STEP_TILES = UNITS // CHUNK_GROUPS
-CHUNK_STEPS = ROW_TILES // STEP_TILES
-STEPS = CHUNKS * CHUNK_STEPS
+STEPS = GROUPS * ROW_TILES // UNITS
+PLAIN_CHUNKS = CHUNKS - 2
 X_BUFS = 10
 W_BUFS = 5
 HALF = 256
@@ -75,6 +74,8 @@ def tile_embed_update_pa_k_kernel(
         nc.gpsimd.memset(wf_plane[:].bitcast(I32), 0)
         token_of = consts.tile([P, P], F32)
         nc.gpsimd.memset(token_of[:], 0.0)
+        token_w = consts.tile([P, P], F32)
+        nc.gpsimd.memset(token_w[:], 0.0)
 
         nc.scalar.dma_start(out=vecs[0:1, 0:HID], in_=b1.rearrange("(o n) -> o n", o=1))
         nc.scalar.dma_start(out=vecs[1:2, 0:CH], in_=b_f.rearrange("(o n) -> o n", o=1))
@@ -95,6 +96,12 @@ def tile_embed_update_pa_k_kernel(
             )
             for place, r in enumerate(tiles):
                 x_place[r, c] = x_raw[:, place, :]
+
+        def load_x_end(r):
+            x_raw = loads.tile([P, 2 * CHUNK_K], BF16, name="x_raw", bufs=X_BUFS)
+            nc.sync.dma_start(out=x_raw[:], in_=x_dram[:, r, PLAIN_CHUNKS * CHUNK_K : K_IN])
+            for place in range(2):
+                x_place[r, PLAIN_CHUNKS + place] = x_raw[:, place * CHUNK_K : (place + 1) * CHUNK_K]
 
         def load_scales(c):
             for q in range(4):
@@ -120,8 +127,8 @@ def tile_embed_update_pa_k_kernel(
                 w_place[first + g] = w_words[:, g, :]
 
         def load_chunk(c):
-            for s in range(CHUNK_STEPS):
-                load_x(c, list(range(s * STEP_TILES, (s + 1) * STEP_TILES)))
+            load_x(c, [0, 1])
+            load_x(c, [2, 3])
             load_scales(c)
             load_w(c * CHUNK_GROUPS, CHUNK_GROUPS)
 
@@ -166,21 +173,23 @@ def tile_embed_update_pa_k_kernel(
         sorted_tiles = {}
         grouped_tiles = {}
 
+        def parts_of(i):
+            plain = 2 * PLAIN_CHUNKS
+            if i < plain:
+                return [(i % 2 * 2 + r, i // 2) for r in range(2)]
+            if i < plain + 2:
+                return [(r, PLAIN_CHUNKS + i - plain) for r in range(2)]
+            return [(i - plain, PLAIN_CHUNKS + c) for c in range(2)]
+
         def units_of(i):
-            c, s = divmod(i, CHUNK_STEPS)
-            return [
-                (s * STEP_TILES + r, c * CHUNK_GROUPS + g)
-                for r in range(STEP_TILES)
-                for g in range(CHUNK_GROUPS)
-            ]
+            return [(r, c * CHUNK_GROUPS + g) for r, c in parts_of(i) for g in range(CHUNK_GROUPS)]
 
         def sort_step(i):
             x_sorted = work.tile([P, UNITS, 2, P], F32, name="x_sorted")
-            c, s = divmod(i, CHUNK_STEPS)
-            for r in range(STEP_TILES):
+            for half, part in enumerate(parts_of(i)):
                 nc.vector.tensor_copy(
-                    out=x_sorted[:, r * CHUNK_GROUPS : (r + 1) * CHUNK_GROUPS, :, :],
-                    in_=x_place[s * STEP_TILES + r, c]
+                    out=x_sorted[:, half * CHUNK_GROUPS : (half + 1) * CHUNK_GROUPS, :, :],
+                    in_=x_place[part]
                     .bitcast(F32)
                     .rearrange("p (g q u) -> p g u q", u=2, q=P),
                 )
@@ -240,9 +249,8 @@ def tile_embed_update_pa_k_kernel(
         h_codes = tail.tile([P, ROW_TILES, P], U32, align_bytes=64)
         h_planes = tail.tile([P, ROW_TILES, P], U8, align_bytes=64)
         gate = tail.tile([P, ROW_TILES], F32)
-        link_l = tail.tile([P, ROW_TILES], F32)
         link_lm = tail.tile([P, ROW_TILES], F32)
-        link_lms = tail.tile([P, ROW_TILES], F32)
+        link_cols = tail.tile([P, 2, ROW_TILES], F32)
         m_f32 = consts.tile([P, ROW_TILES], F32)
         m_sq = consts.tile([P, ROW_TILES], F32)
         m_eps = consts.tile([P, ROW_TILES], F32)
@@ -265,7 +273,7 @@ def tile_embed_update_pa_k_kernel(
         def relu_hidden(r):
             h_out = h_grouped[:, r, :].rearrange("p (j u e) -> p j u e", u=2, e=2)
             h_in = hidden_banks[r][:, 0 : 2 * P].bitcast(BF16).rearrange("p (u j e) -> p j u e", u=2, e=2)
-            if r < ROW_TILES - 1:
+            if r % 2 == 1:
                 nc.scalar.activation(out=h_out, in_=h_in, func=ACT.Relu)
             else:
                 nc.vector.tensor_scalar(out=h_out, in0=h_in, scalar1=0.0, scalar2=None, op0=ALU.max)
@@ -295,8 +303,6 @@ def tile_embed_update_pa_k_kernel(
                 func=ACT.Sigmoid,
                 bias=bf_all[:, FEAT:CH],
             )
-
-        def link_weight(r):
             nc.vector.tensor_scalar(
                 out=link_lm[:, r : r + 1],
                 in0=gate[:, r : r + 1],
@@ -306,53 +312,64 @@ def tile_embed_update_pa_k_kernel(
                 op1=ALU.add,
             )
 
+        def count_links(r):
+            nc.gpsimd.tensor_scalar(
+                out=link_cols[:, 0, r : r + 1],
+                in0=gate[:, r : r + 1],
+                scalar1=m_f32[:, r : r + 1],
+                scalar2=LINK_EPS,
+                op0=ALU.mult,
+                op1=ALU.add,
+            )
+            nc.gpsimd.tensor_tensor(
+                out=link_cols[:, 1, r : r + 1],
+                in0=link_lm[:, r : r + 1],
+                in1=gate[:, r : r + 1],
+                op=ALU.mult,
+            )
+
         weighted = {}
 
-        def weigh(r, onto, first, last):
+        def weigh(r, o, onto, first, last):
             if first == 0:
                 weighted[r] = tail.tile([P, FEAT], F32, name="weighted%d" % r)
             nc.vector.scalar_tensor_tensor(
                 out=weighted[r][:, first:last],
-                in0=o_sum[r][:, first:last],
+                in0=o[:, first:last],
                 scalar=link_lm[:, r : r + 1],
                 in1=weighted[onto][:, first:last],
                 op0=ALU.mult,
                 op1=ALU.add,
             )
 
-        def keep_warm(idle, count):
-            for j in range(count):
-                nc.tensor.matmul(out=idle[:], lhsT=ident_bf[:], rhs=vecs[:], start=True, stop=True)
+        def keep_warm(idle):
+            nc.tensor.matmul(out=idle[:], lhsT=ident_bf[:], rhs=vecs[:], start=True, stop=True)
 
-        def multiply(i):
-            quantise_step(i, 0)
-            quantise_step(i, 1)
-            multiply_step(i)
-
+        last = STEPS - 1
         sort_step(0)
-        transpose_step(0)
-        sort_step(1)
-        transpose_step(1)
-        load_chunk(4)
-        load_chunk(5)
-        multiply(0)
-        multiply(1)
-        sort_step(2)
-        transpose_step(2)
-        sort_step(3)
-        for i in range(3, STEPS):
+        for i in range(STEPS):
             transpose_step(i)
-            multiply(i - 1)
-            if i + 1 < STEPS:
+            if i >= 1:
+                quantise_step(i - 1, 0)
+                quantise_step(i - 1, 1)
+            if i == last:
+                for r in (0, 1):
+                    add_bias(r)
+                    transpose_hidden(r)
+            if i >= 1:
+                multiply_step(i - 1)
+            if i < last:
                 sort_step(i + 1)
+
+            if i == 0:
+                load_chunk(4)
+                load_chunk(5)
             if i == 4:
-                load_chunk(6)
-            if i == 8:
-                nc.vector.tensor_copy(out=m_f32[:], in_=m_bf[:])
-                nc.vector.tensor_tensor(out=m_sq[:], in0=m_f32[:], in1=m_f32[:], op=ALU.mult)
-                nc.vector.tensor_scalar(
-                    out=m_eps[:], in0=m_f32[:], scalar1=LINK_EPS, scalar2=None, op0=ALU.mult
-                )
+                for c in (6, 7):
+                    load_x(c, [0, 1])
+                for c in (6, 7):
+                    load_scales(c)
+                load_w(6 * CHUNK_GROUPS, CHUNK_GROUPS)
             if i == 6:
                 for q in range(4):
                     nc.sync.dma_start(
@@ -363,82 +380,96 @@ def tile_embed_update_pa_k_kernel(
                     out=wf_words[:].bitcast(I32),
                     in_=Wf_words[0].rearrange("p n t -> p (n t)").bitcast(I32),
                 )
-                load_chunk(7)
-        multiply(STEPS - 1)
+                load_x_end(2)
+                load_w(7 * CHUNK_GROUPS, CHUNK_GROUPS)
+                load_x_end(3)
+            if i == 8:
+                nc.vector.tensor_copy(out=m_f32[:], in_=m_bf[:])
+                nc.vector.tensor_tensor(out=m_sq[:], in0=m_f32[:], in1=m_f32[:], op=ALU.mult)
+                nc.vector.tensor_scalar(
+                    out=m_eps[:], in0=m_f32[:], scalar1=LINK_EPS, scalar2=None, op0=ALU.mult
+                )
 
-        for r in range(ROW_TILES):
-            add_bias(r)
-            transpose_hidden(r)
-        keep_warm(sums.tile([P, CH], F32, name="idle0", tag="sum0"), 1)
         relu_hidden(0)
         relu_hidden(1)
-        relu_hidden(2)
-        quantise_hidden(0)
-        multiply_hidden(0)
-        score_links(0)
-        keep_warm(sums.tile([P, CH], F32, name="idle1", tag="sum1"), 1)
-        relu_hidden(3)
-        for r in (1, 3, 2):
+        for r in (0, 1):
+            quantise_step(last, r)
             quantise_hidden(r)
             multiply_hidden(r)
+        add_bias(2)
+        for r in (0, 1):
             score_links(r)
-        keep_warm(banks.tile([P, CH], F32, name="bank"), 3)
+            count_links(r)
+        weighted[1] = tail.tile([P, FEAT], F32, name="weighted1")
+        nc.scalar.activation(
+            out=weighted[1][:], in_=o_sum[1][:, 0:FEAT], func=ACT.Copy, scale=link_lm[:, 1:2]
+        )
+        weigh(0, o_sum[0], 1, 0, FEAT)
+        multiply_step(last)
 
-        pooled = [banks.tile([P, 4 * P], F32, name="bank") for j in range(2)]
+        add_bias(3)
+        transpose_hidden(2)
+        transpose_hidden(3)
+        idle = sums.tile([P, CH], F32, name="idle", tag="sum3")
+        keep_warm(idle)
+        relu_hidden(2)
+        relu_hidden(3)
+        quantise_hidden(2)
+        multiply_hidden(2)
+        keep_warm(idle)
+        quantise_hidden(3)
+        multiply_hidden(3)
+
         halves = [(0, HALF), (HALF, FEAT)]
+        pooled = [banks.tile([P, 4 * P], F32, name="bank") for j in range(2)]
 
-        def pool_half(r, j):
-            first, last = halves[j]
+        def pool_half(j, weights, rows, opens):
+            first, last_col = halves[j]
             nc.tensor.matmul(
-                out=pooled[j][:, 0 : last - first],
-                lhsT=token_of[:],
-                rhs=weighted[r][:, first:last],
-                start=(r == ROW_TILES - 1),
-                stop=(r != ROW_TILES - 1),
+                out=pooled[j][:, 0 : last_col - first],
+                lhsT=weights[:],
+                rhs=rows[:, first:last_col],
+                start=opens,
+                stop=not opens,
             )
 
-        link_weight(0)
-        weighted[0] = tail.tile([P, FEAT], F32, name="weighted0")
+        score_links(2)
+        count_links(2)
+        lm_sum = tail.tile([P, 1], F32)
+        nc.vector.tensor_reduce(out=lm_sum[:], in_=link_lm[:, 0:3], axis=AXIS.X, op=ALU.add)
         nc.vector.tensor_scalar(
-            out=weighted[0][:],
-            in0=o_sum[0][:, 0:FEAT],
-            scalar1=link_lm[:, 0:1],
+            out=token_w[:, 0:TOKENS],
+            in0=token_of[:, 0:TOKENS],
+            scalar1=lm_sum[:],
             scalar2=None,
             op0=ALU.mult,
         )
-        link_weight(1)
-        link_weight(3)
-        weighted[3] = tail.tile([P, FEAT], F32, name="weighted3")
-        nc.scalar.activation(
-            out=weighted[3][:], in_=o_sum[3][:, 0:FEAT], func=ACT.Copy, scale=link_lm[:, 3:4]
+        for j in range(2):
+            pool_half(j, token_w, bf_all, True)
+        weigh(2, o_sum[2], 0, 0, FEAT)
+        o_last = tail.tile([P, FEAT], F32)
+        nc.vector.tensor_tensor(
+            out=o_last[:], in0=o_sum[3][:, 0:FEAT], in1=bf_all[:, 0:FEAT], op=ALU.add
         )
-        weigh(1, 0, 0, FEAT)
-        link_weight(2)
+        score_links(3)
+        count_links(3)
         nc.scalar.activation(out=warm[:], in_=eps_col[:], func=ACT.Abs_reciprocal_sqrt)
-        nc.gpsimd.tensor_tensor(out=link_l[:], in0=gate[:], in1=m_f32[:], op=ALU.mult)
-        nc.gpsimd.tensor_tensor(out=link_lms[:], in0=link_lm[:], in1=gate[:], op=ALU.mult)
-        nc.gpsimd.tensor_scalar(
-            out=link_l[:], in0=link_l[:], scalar1=1.0, scalar2=LINK_EPS, op0=ALU.mult, op1=ALU.add
+        link_sum = banks.tile([P, 4 * P], F32, name="bank")
+        nc.tensor.matmul(
+            out=link_sum[:, 0 : 2 * ROW_TILES],
+            lhsT=token_of[:],
+            rhs=link_cols[:].rearrange("p j r -> p (j r)"),
+            start=True,
+            stop=True,
         )
         for j in range(2):
-            pool_half(3, j)
-        link_sum = banks.tile([P, 4 * P], F32, name="bank")
-        for j, cols in enumerate((link_l, link_lm, link_lms)):
-            nc.tensor.matmul(
-                out=link_sum[:, j * ROW_TILES : (j + 1) * ROW_TILES],
-                lhsT=token_of[:],
-                rhs=cols[:],
-                start=True,
-                stop=True,
-            )
-        for j in range(2):
-            weigh(2, 1, halves[j][0], halves[j][1])
-            pool_half(2, j)
+            weigh(3, o_last, 2, halves[j][0], halves[j][1])
+            pool_half(j, token_of, weighted[3], False)
 
-        total = tail.tile([TOKENS, 3], F32)
+        total = tail.tile([TOKENS, 2], F32)
         nc.vector.tensor_reduce(
             out=total[:],
-            in_=link_sum[0:TOKENS, 0 : 3 * ROW_TILES].rearrange("p (j r) -> p j r", r=ROW_TILES),
+            in_=link_sum[0:TOKENS, 0 : 2 * ROW_TILES].rearrange("p (j r) -> p j r", r=ROW_TILES),
             axis=AXIS.X,
             op=ALU.add,
         )
@@ -446,20 +477,7 @@ def tile_embed_update_pa_k_kernel(
         nc.vector.reciprocal(out=inv[:], in_=total[:, 0:1])
         gain = tail.tile([TOKENS, 1], F32)
         nc.vector.tensor_scalar(
-            out=gain[:], in0=total[:, 2:3], scalar1=inv[:], scalar2=inv[:], op0=ALU.mult, op1=ALU.mult
-        )
-        bias_gain = tail.tile([TOKENS, 1], F32)
-        nc.vector.tensor_scalar(
-            out=bias_gain[:], in0=total[:, 1:2], scalar1=gain[:], scalar2=None, op0=ALU.mult
-        )
-        base = tail.tile([TOKENS, FEAT], F32)
-        nc.vector.scalar_tensor_tensor(
-            out=base[:],
-            in0=bf_all[0:TOKENS, 0:FEAT],
-            scalar=bias_gain[:],
-            in1=emb[:],
-            op0=ALU.mult,
-            op1=ALU.add,
+            out=gain[:], in0=total[:, 1:2], scalar1=inv[:], scalar2=inv[:], op0=ALU.mult, op1=ALU.mult
         )
         e = tail.tile([TOKENS, FEAT], F32)
         stats = tail.tile([TOKENS, 2, 6], F32)
@@ -468,7 +486,7 @@ def tile_embed_update_pa_k_kernel(
                 out=e[:, first:last],
                 in0=pooled[j][0:TOKENS, 0 : last - first],
                 scalar=gain[:],
-                in1=base[:, first:last],
+                in1=emb[:, first:last],
                 op0=ALU.mult,
                 op1=ALU.add,
             )

@@ -61,15 +61,19 @@ def tile_embed_update_pa_k_kernel(
         nc.vector.memset(vecs[:].bitcast(I32), 0)
         w1_planes = consts.tile([P, CHUNKS, HID], U8, align_bytes=256)
         nc.vector.memset(w1_planes[:, 0, :].bitcast(I32), 0)
+        zero_rows = consts.tile([P, CH], BF16)
+        nc.vector.memset(zero_rows[:].bitcast(I32), 0)
         zero_col = consts.tile([P, 1], F32)
         nc.vector.memset(zero_col[:], 0.0)
-        nc.vector.memset(w1_planes[:, 1:CHUNKS, :].bitcast(I32), 0)
         ident_f32 = consts.tile([P, P], F32)
         make_identity(nc, ident_f32[:])
+        ident_bf = consts.tile([P, P], BF16)
+        nc.vector.tensor_copy(out=ident_bf[:], in_=ident_f32[:])
         eps_col = consts.tile([P, 1], F32)
         nc.vector.tensor_scalar(
             out=eps_col[:], in0=zero_col[:], scalar1=1.0, scalar2=LN_EPS, op0=ALU.mult, op1=ALU.add
         )
+        nc.vector.memset(w1_planes[:, 1:CHUNKS, :].bitcast(I32), 0)
         wf_plane = consts.tile([P, CH], U8, align_bytes=256)
         nc.gpsimd.memset(wf_plane[:].bitcast(I32), 0)
         token_of = consts.tile([P, P], F32)
@@ -146,8 +150,6 @@ def tile_embed_update_pa_k_kernel(
         emb = consts.tile([TOKENS, FEAT], BF16)
         nc.sync.dma_start(out=emb[:], in_=embeds.rearrange("b s c -> (b s) c"))
 
-        ident_bf = consts.tile([P, P], BF16)
-        nc.vector.tensor_copy(out=ident_bf[:], in_=ident_f32[:])
         nc.vector.tensor_reduce(
             out=token_of[:, 0:TOKENS],
             in_=ident_f32[:].rearrange("p (j i) -> p j i", i=LINK_PARTS),
@@ -155,21 +157,26 @@ def tile_embed_update_pa_k_kernel(
             op=ALU.add,
         )
         spread = []
-        for j in range(4):
-            picked = sums.tile([P, CH], F32, name="picked", tag="sum%d" % j)
-            nc.tensor.matmul(
-                out=picked[:],
-                lhsT=ident_bf[:, j : j + 1].to_broadcast([P, P]),
-                rhs=vecs[:],
-                start=True,
-                stop=True,
-            )
-            row = consts.tile([P, CH], F32, name="spread%d" % j)
-            nc.scalar.copy(out=row[:], in_=picked[:])
-            spread.append(row)
-        b1_all, bf_all, gamma_all, beta_all = spread
 
-        acc = [sums.tile([P, HID], F32, name="acc%d" % r, tag="sum%d" % r) for r in range(ROW_TILES)]
+        def spread_vectors():
+            for j in range(4):
+                picked = sums.tile([P, CH], F32, name="picked", tag="sum%d" % j)
+                nc.tensor.matmul(
+                    out=picked[:],
+                    lhsT=ident_bf[:, j : j + 1].to_broadcast([P, P]),
+                    rhs=vecs[:],
+                    start=True,
+                    stop=True,
+                )
+                row = consts.tile([P, CH], F32, name="spread%d" % j)
+                nc.scalar.copy(out=row[:], in_=picked[:])
+                spread.append(row)
+
+        def keep_warm(idle, count):
+            for j in range(count):
+                nc.tensor.matmul(out=idle[:], lhsT=ident_bf[:], rhs=zero_rows[:], start=True, stop=True)
+
+        acc = {}
         sorted_tiles = {}
         grouped_tiles = {}
 
@@ -250,14 +257,15 @@ def tile_embed_update_pa_k_kernel(
         h_planes = tail.tile([P, ROW_TILES, P], U8, align_bytes=64)
         gate = tail.tile([P, ROW_TILES], F32)
         link_lm = tail.tile([P, ROW_TILES], F32)
-        link_cols = tail.tile([P, 2, ROW_TILES], F32)
+        link_l = tail.tile([P, ROW_TILES], F32)
+        link_lms = tail.tile([P, ROW_TILES], F32)
         m_f32 = consts.tile([P, ROW_TILES], F32)
         m_sq = consts.tile([P, ROW_TILES], F32)
         m_eps = consts.tile([P, ROW_TILES], F32)
         o_sum = {}
 
         def add_bias(r):
-            nc.vector.tensor_tensor(out=pre_h[:, r, :], in0=acc[r][:], in1=b1_all[:], op=ALU.add)
+            nc.vector.tensor_tensor(out=pre_h[:, r, :], in0=acc[r][:], in1=spread[0][:], op=ALU.add)
 
         hidden_banks = {}
 
@@ -273,7 +281,7 @@ def tile_embed_update_pa_k_kernel(
         def relu_hidden(r):
             h_out = h_grouped[:, r, :].rearrange("p (j u e) -> p j u e", u=2, e=2)
             h_in = hidden_banks[r][:, 0 : 2 * P].bitcast(BF16).rearrange("p (u j e) -> p j u e", u=2, e=2)
-            if r % 2 == 1:
+            if r % 2 == 0:
                 nc.scalar.activation(out=h_out, in_=h_in, func=ACT.Relu)
             else:
                 nc.vector.tensor_scalar(out=h_out, in0=h_in, scalar1=0.0, scalar2=None, op0=ALU.max)
@@ -301,8 +309,10 @@ def tile_embed_update_pa_k_kernel(
                 out=gate[:, r : r + 1],
                 in_=o_sum[r][:, FEAT:CH],
                 func=ACT.Sigmoid,
-                bias=bf_all[:, FEAT:CH],
+                bias=spread[1][:, FEAT:CH],
             )
+
+        def link_weight(r):
             nc.vector.tensor_scalar(
                 out=link_lm[:, r : r + 1],
                 in0=gate[:, r : r + 1],
@@ -313,19 +323,19 @@ def tile_embed_update_pa_k_kernel(
             )
 
         def count_links(r):
+            nc.vector.tensor_tensor(
+                out=link_lms[:, r : r + 1],
+                in0=link_lm[:, r : r + 1],
+                in1=gate[:, r : r + 1],
+                op=ALU.mult,
+            )
             nc.gpsimd.tensor_scalar(
-                out=link_cols[:, 0, r : r + 1],
+                out=link_l[:, r : r + 1],
                 in0=gate[:, r : r + 1],
                 scalar1=m_f32[:, r : r + 1],
                 scalar2=LINK_EPS,
                 op0=ALU.mult,
                 op1=ALU.add,
-            )
-            nc.gpsimd.tensor_tensor(
-                out=link_cols[:, 1, r : r + 1],
-                in0=link_lm[:, r : r + 1],
-                in1=gate[:, r : r + 1],
-                op=ALU.mult,
             )
 
         weighted = {}
@@ -342,13 +352,16 @@ def tile_embed_update_pa_k_kernel(
                 op1=ALU.add,
             )
 
-        def keep_warm(idle):
-            nc.tensor.matmul(out=idle[:], lhsT=ident_bf[:], rhs=vecs[:], start=True, stop=True)
-
         last = STEPS - 1
+        keep_warm(sums.tile([P, CH], F32, name="idle", tag="sum3"), 6)
         sort_step(0)
         for i in range(STEPS):
             transpose_step(i)
+            if i == 0:
+                spread_vectors()
+                b1_all, bf_all, gamma_all, beta_all = spread
+                for r in range(ROW_TILES):
+                    acc[r] = sums.tile([P, HID], F32, name="acc%d" % r, tag="sum%d" % r)
             if i >= 1:
                 quantise_step(i - 1, 0)
                 quantise_step(i - 1, 1)
@@ -363,14 +376,6 @@ def tile_embed_update_pa_k_kernel(
 
             if i == 0:
                 load_chunk(4)
-                load_chunk(5)
-            if i == 4:
-                for c in (6, 7):
-                    load_x(c, [0, 1])
-                for c in (6, 7):
-                    load_scales(c)
-                load_w(6 * CHUNK_GROUPS, CHUNK_GROUPS)
-            if i == 6:
                 for q in range(4):
                     nc.sync.dma_start(
                         out=wf_plane[32 * q : 32 * q + 4, :].bitcast(I32),
@@ -380,6 +385,14 @@ def tile_embed_update_pa_k_kernel(
                     out=wf_words[:].bitcast(I32),
                     in_=Wf_words[0].rearrange("p n t -> p (n t)").bitcast(I32),
                 )
+                load_chunk(5)
+            if i == 4:
+                load_x(6, [0, 1])
+                load_scales(6)
+                load_w(6 * CHUNK_GROUPS, CHUNK_GROUPS)
+                load_x(7, [0, 1])
+                load_scales(7)
+            if i == 6:
                 load_x_end(2)
                 load_w(7 * CHUNK_GROUPS, CHUNK_GROUPS)
                 load_x_end(3)
@@ -399,6 +412,7 @@ def tile_embed_update_pa_k_kernel(
         add_bias(2)
         for r in (0, 1):
             score_links(r)
+            link_weight(r)
             count_links(r)
         weighted[1] = tail.tile([P, FEAT], F32, name="weighted1")
         nc.scalar.activation(
@@ -411,14 +425,16 @@ def tile_embed_update_pa_k_kernel(
         transpose_hidden(2)
         transpose_hidden(3)
         idle = sums.tile([P, CH], F32, name="idle", tag="sum3")
-        keep_warm(idle)
+        keep_warm(idle, 1)
         relu_hidden(2)
-        relu_hidden(3)
         quantise_hidden(2)
+        relu_hidden(3)
         multiply_hidden(2)
-        keep_warm(idle)
+        score_links(2)
+        keep_warm(idle, 1)
         quantise_hidden(3)
         multiply_hidden(3)
+        score_links(3)
 
         halves = [(0, HALF), (HALF, FEAT)]
         pooled = [banks.tile([P, 4 * P], F32, name="bank") for j in range(2)]
@@ -433,7 +449,7 @@ def tile_embed_update_pa_k_kernel(
                 stop=not opens,
             )
 
-        score_links(2)
+        link_weight(2)
         count_links(2)
         lm_sum = tail.tile([P, 1], F32)
         nc.vector.tensor_reduce(out=lm_sum[:], in_=link_lm[:, 0:3], axis=AXIS.X, op=ALU.add)
@@ -451,17 +467,18 @@ def tile_embed_update_pa_k_kernel(
         nc.vector.tensor_tensor(
             out=o_last[:], in0=o_sum[3][:, 0:FEAT], in1=bf_all[:, 0:FEAT], op=ALU.add
         )
-        score_links(3)
+        link_weight(3)
         count_links(3)
         nc.scalar.activation(out=warm[:], in_=eps_col[:], func=ACT.Abs_reciprocal_sqrt)
         link_sum = banks.tile([P, 4 * P], F32, name="bank")
-        nc.tensor.matmul(
-            out=link_sum[:, 0 : 2 * ROW_TILES],
-            lhsT=token_of[:],
-            rhs=link_cols[:].rearrange("p j r -> p (j r)"),
-            start=True,
-            stop=True,
-        )
+        for j, cols in enumerate((link_l, link_lms)):
+            nc.tensor.matmul(
+                out=link_sum[:, j * ROW_TILES : (j + 1) * ROW_TILES],
+                lhsT=token_of[:],
+                rhs=cols[:],
+                start=True,
+                stop=True,
+            )
         for j in range(2):
             weigh(3, o_last, 2, halves[j][0], halves[j][1])
             pool_half(j, token_of, weighted[3], False)
@@ -502,21 +519,23 @@ def tile_embed_update_pa_k_kernel(
             bias=eps_col[0:TOKENS, :],
         )
         centred = tail.tile([TOKENS, FEAT], F32)
-        nc.vector.scalar_tensor_tensor(
-            out=centred[:],
-            in0=e[:],
-            scalar=mean_var[:, 0:1],
-            in1=gamma_all[0:TOKENS, 0:FEAT],
-            op0=ALU.subtract,
-            op1=ALU.mult,
-        )
+        for first, last in halves:
+            nc.vector.scalar_tensor_tensor(
+                out=centred[:, first:last],
+                in0=e[:, first:last],
+                scalar=mean_var[:, 0:1],
+                in1=gamma_all[0:TOKENS, first:last],
+                op0=ALU.subtract,
+                op1=ALU.mult,
+            )
         y = tail.tile([TOKENS, FEAT], F32)
-        nc.vector.scalar_tensor_tensor(
-            out=y[:],
-            in0=centred[:],
-            scalar=rstd[:],
-            in1=beta_all[0:TOKENS, 0:FEAT],
-            op0=ALU.mult,
-            op1=ALU.add,
-        )
+        for first, last in halves:
+            nc.vector.scalar_tensor_tensor(
+                out=y[:, first:last],
+                in0=centred[:, first:last],
+                scalar=rstd[:],
+                in1=beta_all[0:TOKENS, first:last],
+                op0=ALU.mult,
+                op1=ALU.add,
+            )
         nc.sync.dma_start(out=out.rearrange("b s c -> (b s) c"), in_=y[:])

@@ -31,7 +31,6 @@ CHUNK_GROUPS = 4
 CHUNKS = GROUPS // CHUNK_GROUPS
 CHUNK_K = CHUNK_GROUPS * K_PASS
 STEPS = GROUPS * ROW_TILES // UNITS
-PLAIN_CHUNKS = CHUNKS - 2
 X_BUFS = 10
 W_BUFS = 5
 HALF = 256
@@ -78,8 +77,6 @@ def tile_embed_update_pa_k_kernel(
         nc.gpsimd.memset(wf_plane[:].bitcast(I32), 0)
         token_of = consts.tile([P, P], F32)
         nc.gpsimd.memset(token_of[:], 0.0)
-        token_w = consts.tile([P, P], F32)
-        nc.gpsimd.memset(token_w[:], 0.0)
 
         nc.scalar.dma_start(out=vecs[0:1, 0:HID], in_=b1.rearrange("(o n) -> o n", o=1))
         nc.scalar.dma_start(out=vecs[1:2, 0:CH], in_=b_f.rearrange("(o n) -> o n", o=1))
@@ -100,12 +97,6 @@ def tile_embed_update_pa_k_kernel(
             )
             for place, r in enumerate(tiles):
                 x_place[r, c] = x_raw[:, place, :]
-
-        def load_x_end(r):
-            x_raw = loads.tile([P, 2 * CHUNK_K], BF16, name="x_raw", bufs=X_BUFS)
-            nc.sync.dma_start(out=x_raw[:], in_=x_dram[:, r, PLAIN_CHUNKS * CHUNK_K : K_IN])
-            for place in range(2):
-                x_place[r, PLAIN_CHUNKS + place] = x_raw[:, place * CHUNK_K : (place + 1) * CHUNK_K]
 
         def load_scales(c):
             for q in range(4):
@@ -181,12 +172,7 @@ def tile_embed_update_pa_k_kernel(
         grouped_tiles = {}
 
         def parts_of(i):
-            plain = 2 * PLAIN_CHUNKS
-            if i < plain:
-                return [(i % 2 * 2 + r, i // 2) for r in range(2)]
-            if i < plain + 2:
-                return [(r, PLAIN_CHUNKS + i - plain) for r in range(2)]
-            return [(i - plain, PLAIN_CHUNKS + c) for c in range(2)]
+            return [(i % 2 * 2 + r, i // 2) for r in range(2)]
 
         def units_of(i):
             return [(r, c * CHUNK_GROUPS + g) for r, c in parts_of(i) for g in range(CHUNK_GROUPS)]
@@ -202,7 +188,7 @@ def tile_embed_update_pa_k_kernel(
                 )
             sorted_tiles[i] = x_sorted
 
-        def transpose_step(i):
+        def transpose_step(i, vector_bank):
             x_sorted = sorted_tiles[i]
             grouped = work.tile([P, UNITS, K_PASS], BF16, name="grouped", align_bytes=256)
             grouped_words = grouped[:].bitcast(F32)
@@ -215,10 +201,12 @@ def tile_embed_update_pa_k_kernel(
                             x_sorted[:, k + k2, u, :],
                             ident_f32[:],
                         )
-                nc.scalar.copy(
-                    out=grouped_words[:, k : k + 2, :].rearrange("p k (j u) -> p k j u", u=2),
-                    in_=bank[:].rearrange("p (k u j) -> p k j u", k=2, u=2),
-                )
+                words_out = grouped_words[:, k : k + 2, :].rearrange("p k (j u) -> p k j u", u=2)
+                words_in = bank[:].rearrange("p (k u j) -> p k j u", k=2, u=2)
+                if k // 2 == vector_bank:
+                    nc.vector.tensor_copy(out=words_out, in_=words_in)
+                else:
+                    nc.scalar.copy(out=words_out, in_=words_in)
             grouped_tiles[i] = grouped
 
         code_tiles = {}
@@ -236,9 +224,10 @@ def tile_embed_update_pa_k_kernel(
                 in_=grouped_tiles[i][:, units, :].rearrange("p k j -> p (k j)"),
             )
 
-        def multiply_step(i):
+        def multiply_part(i, part):
             x_codes, x_planes = code_tiles[i]
-            for k, (r, group) in enumerate(units_of(i)):
+            for k in range(part * CHUNK_GROUPS, (part + 1) * CHUNK_GROUPS):
+                r, group = units_of(i)[k]
                 c, j = divmod(group, CHUNK_GROUPS)
                 nc.tensor.matmul_mx(
                     out=acc[r][:],
@@ -353,26 +342,29 @@ def tile_embed_update_pa_k_kernel(
             )
 
         last = STEPS - 1
+        runs = [([0, 1], [0]), ([2], [1]), ([3], [2, 3])]
+        runs += [([i, i + 1], [i, i + 1]) for i in range(4, STEPS, 2)]
         keep_warm(sums.tile([P, CH], F32, name="idle", tag="sum3"), 6)
         sort_step(0)
-        for i in range(STEPS):
-            transpose_step(i)
-            if i == 0:
-                spread_vectors()
-                b1_all, bf_all, gamma_all, beta_all = spread
-                for r in range(ROW_TILES):
-                    acc[r] = sums.tile([P, HID], F32, name="acc%d" % r, tag="sum%d" % r)
-            if i >= 1:
-                quantise_step(i - 1, 0)
-                quantise_step(i - 1, 1)
-            if i == last:
-                for r in (0, 1):
-                    add_bias(r)
-                    transpose_hidden(r)
-            if i >= 1:
-                multiply_step(i - 1)
-            if i < last:
-                sort_step(i + 1)
+        sort_step(1)
+        for n, (to_transpose, to_multiply) in enumerate(runs):
+            for i in to_transpose:
+                transpose_step(i, 2 if i >= 4 and i == to_transpose[0] else -1)
+                if i == 0:
+                    spread_vectors()
+                    b1_all, bf_all, gamma_all, beta_all = spread
+                    for r in range(ROW_TILES):
+                        acc[r] = sums.tile([P, HID], F32, name="acc%d" % r, tag="sum%d" % r)
+            for i in to_multiply:
+                for part in range(2):
+                    quantise_step(i, part)
+            if last not in to_multiply:
+                for i in to_multiply:
+                    for part in range(2):
+                        multiply_part(i, part)
+                for i in runs[n + 1][0]:
+                    sort_step(i)
+            i = to_multiply[-1]
 
             if i == 0:
                 load_chunk(4)
@@ -386,92 +378,67 @@ def tile_embed_update_pa_k_kernel(
                     in_=Wf_words[0].rearrange("p n t -> p (n t)").bitcast(I32),
                 )
                 load_chunk(5)
-            if i == 4:
-                load_x(6, [0, 1])
-                load_scales(6)
-                load_w(6 * CHUNK_GROUPS, CHUNK_GROUPS)
-                load_x(7, [0, 1])
-                load_scales(7)
-            if i == 6:
-                load_x_end(2)
-                load_w(7 * CHUNK_GROUPS, CHUNK_GROUPS)
-                load_x_end(3)
-            if i == 8:
+            if i == 3:
+                load_chunk(6)
+            if i == 5:
+                load_chunk(7)
+            if i == 9:
                 nc.vector.tensor_copy(out=m_f32[:], in_=m_bf[:])
                 nc.vector.tensor_tensor(out=m_sq[:], in0=m_f32[:], in1=m_f32[:], op=ALU.mult)
                 nc.vector.tensor_scalar(
                     out=m_eps[:], in0=m_f32[:], scalar1=LINK_EPS, scalar2=None, op0=ALU.mult
                 )
 
+        for r in range(3):
+            multiply_part(last - 1 + r // 2, r % 2)
+            add_bias(r)
+        transpose_hidden(0)
+        transpose_hidden(1)
         relu_hidden(0)
         relu_hidden(1)
+        multiply_part(last, 1)
         for r in (0, 1):
-            quantise_step(last, r)
             quantise_hidden(r)
             multiply_hidden(r)
-        add_bias(2)
-        for r in (0, 1):
-            score_links(r)
-            link_weight(r)
-            count_links(r)
-        weighted[1] = tail.tile([P, FEAT], F32, name="weighted1")
-        nc.scalar.activation(
-            out=weighted[1][:], in_=o_sum[1][:, 0:FEAT], func=ACT.Copy, scale=link_lm[:, 1:2]
-        )
-        weigh(0, o_sum[0], 1, 0, FEAT)
-        multiply_step(last)
-
         add_bias(3)
         transpose_hidden(2)
         transpose_hidden(3)
         idle = sums.tile([P, CH], F32, name="idle", tag="sum3")
-        keep_warm(idle, 1)
-        relu_hidden(2)
-        quantise_hidden(2)
-        relu_hidden(3)
-        multiply_hidden(2)
-        score_links(2)
-        keep_warm(idle, 1)
-        quantise_hidden(3)
-        multiply_hidden(3)
-        score_links(3)
-
-        halves = [(0, HALF), (HALF, FEAT)]
-        pooled = [banks.tile([P, 4 * P], F32, name="bank") for j in range(2)]
-
-        def pool_half(j, weights, rows, opens):
-            first, last_col = halves[j]
-            nc.tensor.matmul(
-                out=pooled[j][:, 0 : last_col - first],
-                lhsT=weights[:],
-                rhs=rows[:, first:last_col],
-                start=opens,
-                stop=not opens,
-            )
-
-        link_weight(2)
-        count_links(2)
-        lm_sum = tail.tile([P, 1], F32)
-        nc.vector.tensor_reduce(out=lm_sum[:], in_=link_lm[:, 0:3], axis=AXIS.X, op=ALU.add)
+        keep_warm(idle, 2)
+        score_links(0)
+        score_links(1)
+        link_weight(0)
+        count_links(0)
+        weighted[0] = tail.tile([P, FEAT], F32, name="weighted0")
         nc.vector.tensor_scalar(
-            out=token_w[:, 0:TOKENS],
-            in0=token_of[:, 0:TOKENS],
-            scalar1=lm_sum[:],
+            out=weighted[0][:],
+            in0=o_sum[0][:, 0:FEAT],
+            scalar1=link_lm[:, 0:1],
             scalar2=None,
             op0=ALU.mult,
         )
-        for j in range(2):
-            pool_half(j, token_w, bf_all, True)
-        weigh(2, o_sum[2], 0, 0, FEAT)
-        o_last = tail.tile([P, FEAT], F32)
-        nc.vector.tensor_tensor(
-            out=o_last[:], in0=o_sum[3][:, 0:FEAT], in1=bf_all[:, 0:FEAT], op=ALU.add
-        )
+        relu_hidden(2)
+        relu_hidden(3)
+        link_weight(1)
+        count_links(1)
+        quantise_hidden(2)
+        multiply_hidden(2)
+        quantise_hidden(3)
+        multiply_hidden(3)
+        score_links(2)
+        score_links(3)
+        keep_warm(banks.tile([P, CH], F32, name="bank"), 3)
+
+        halves = [(0, HALF), (HALF, FEAT)]
+        weigh(1, o_sum[1], 0, 0, FEAT)
+        link_weight(2)
+        count_links(2)
+        weigh(2, o_sum[2], 1, 0, FEAT)
         link_weight(3)
         count_links(3)
         nc.scalar.activation(out=warm[:], in_=eps_col[:], func=ACT.Abs_reciprocal_sqrt)
         link_sum = banks.tile([P, 4 * P], F32, name="bank")
-        for j, cols in enumerate((link_l, link_lms)):
+        for j, cols in enumerate((link_l, link_lm, link_lms)):
             nc.tensor.matmul(
                 out=link_sum[:, j * ROW_TILES : (j + 1) * ROW_TILES],
                 lhsT=token_of[:],
@@ -479,14 +446,23 @@ def tile_embed_update_pa_k_kernel(
                 start=True,
                 stop=True,
             )
-        for j in range(2):
-            weigh(3, o_last, 2, halves[j][0], halves[j][1])
-            pool_half(j, token_of, weighted[3], False)
+        pooled = []
+        for first, last_col in halves:
+            weigh(3, o_sum[3], 2, first, last_col)
+            half = banks.tile([P, 4 * P], F32, name="bank")
+            nc.tensor.matmul(
+                out=half[:, 0 : last_col - first],
+                lhsT=token_of[:],
+                rhs=weighted[3][:, first:last_col],
+                start=True,
+                stop=True,
+            )
+            pooled.append(half)
 
-        total = tail.tile([TOKENS, 2], F32)
+        total = tail.tile([TOKENS, 3], F32)
         nc.vector.tensor_reduce(
             out=total[:],
-            in_=link_sum[0:TOKENS, 0 : 2 * ROW_TILES].rearrange("p (j r) -> p j r", r=ROW_TILES),
+            in_=link_sum[0:TOKENS, 0 : 3 * ROW_TILES].rearrange("p (j r) -> p j r", r=ROW_TILES),
             axis=AXIS.X,
             op=ALU.add,
         )
@@ -494,7 +470,20 @@ def tile_embed_update_pa_k_kernel(
         nc.vector.reciprocal(out=inv[:], in_=total[:, 0:1])
         gain = tail.tile([TOKENS, 1], F32)
         nc.vector.tensor_scalar(
-            out=gain[:], in0=total[:, 1:2], scalar1=inv[:], scalar2=inv[:], op0=ALU.mult, op1=ALU.mult
+            out=gain[:], in0=total[:, 2:3], scalar1=inv[:], scalar2=inv[:], op0=ALU.mult, op1=ALU.mult
+        )
+        bias_gain = tail.tile([TOKENS, 1], F32)
+        nc.vector.tensor_scalar(
+            out=bias_gain[:], in0=total[:, 1:2], scalar1=gain[:], scalar2=None, op0=ALU.mult
+        )
+        base = tail.tile([TOKENS, FEAT], F32)
+        nc.vector.scalar_tensor_tensor(
+            out=base[:],
+            in0=bf_all[0:TOKENS, 0:FEAT],
+            scalar=bias_gain[:],
+            in1=emb[:],
+            op0=ALU.mult,
+            op1=ALU.add,
         )
         e = tail.tile([TOKENS, FEAT], F32)
         stats = tail.tile([TOKENS, 2, 6], F32)
@@ -503,7 +492,7 @@ def tile_embed_update_pa_k_kernel(
                 out=e[:, first:last],
                 in0=pooled[j][0:TOKENS, 0 : last - first],
                 scalar=gain[:],
-                in1=emb[:, first:last],
+                in1=base[:, first:last],
                 op0=ALU.mult,
                 op1=ALU.add,
             )

@@ -17,6 +17,7 @@ P = 128
 ROWS = 512
 ROW_TILES = ROWS // P
 TOKENS = 32
+LINKS = ROWS // TOKENS
 LINK_PARTS = P // TOKENS
 K_IN = 16384
 K_PASS = 512
@@ -77,6 +78,8 @@ def tile_embed_update_pa_k_kernel(
         nc.gpsimd.memset(wf_plane[:].bitcast(I32), 0)
         token_of = consts.tile([P, P], F32)
         nc.gpsimd.memset(token_of[:], 0.0)
+        pool_w = consts.tile([P, P], F32)
+        nc.gpsimd.memset(pool_w[:], 0.0)
 
         nc.scalar.dma_start(out=vecs[0:1, 0:HID], in_=b1.rearrange("(o n) -> o n", o=1))
         nc.scalar.dma_start(out=vecs[1:2, 0:CH], in_=b_f.rearrange("(o n) -> o n", o=1))
@@ -245,9 +248,8 @@ def tile_embed_update_pa_k_kernel(
         h_codes = tail.tile([P, ROW_TILES, P], U32, align_bytes=64)
         h_planes = tail.tile([P, ROW_TILES, P], U8, align_bytes=64)
         gate = tail.tile([P, ROW_TILES], F32)
-        link_lm = tail.tile([P, ROW_TILES], F32)
-        link_l = tail.tile([P, ROW_TILES], F32)
-        link_lms = tail.tile([P, ROW_TILES], F32)
+        link_cols = tail.tile([P, 3, ROW_TILES], F32)
+        link_ms, link_lm, link_lms = [link_cols[:, j, :] for j in range(3)]
         m_f32 = consts.tile([P, ROW_TILES], F32)
         m_sq = consts.tile([P, ROW_TILES], F32)
         m_eps = consts.tile([P, ROW_TILES], F32)
@@ -267,10 +269,10 @@ def tile_embed_update_pa_k_kernel(
                 )
             hidden_banks[r] = bank
 
-        def relu_hidden(r):
+        def relu_hidden(r, on_scalar):
             h_out = h_grouped[:, r, :].rearrange("p (j u e) -> p j u e", u=2, e=2)
             h_in = hidden_banks[r][:, 0 : 2 * P].bitcast(BF16).rearrange("p (u j e) -> p j u e", u=2, e=2)
-            if r % 2 == 0:
+            if on_scalar:
                 nc.scalar.activation(out=h_out, in_=h_in, func=ACT.Relu)
             else:
                 nc.vector.tensor_scalar(out=h_out, in0=h_in, scalar1=0.0, scalar2=None, op0=ALU.max)
@@ -311,22 +313,6 @@ def tile_embed_update_pa_k_kernel(
                 op1=ALU.add,
             )
 
-        def count_links(r):
-            nc.vector.tensor_tensor(
-                out=link_lms[:, r : r + 1],
-                in0=link_lm[:, r : r + 1],
-                in1=gate[:, r : r + 1],
-                op=ALU.mult,
-            )
-            nc.gpsimd.tensor_scalar(
-                out=link_l[:, r : r + 1],
-                in0=gate[:, r : r + 1],
-                scalar1=m_f32[:, r : r + 1],
-                scalar2=LINK_EPS,
-                op0=ALU.mult,
-                op1=ALU.add,
-            )
-
         weighted = {}
 
         def weigh(r, o, onto, first, last):
@@ -342,31 +328,29 @@ def tile_embed_update_pa_k_kernel(
             )
 
         last = STEPS - 1
-        runs = [([0, 1], [0]), ([2], [1]), ([3], [2, 3])]
-        runs += [([i, i + 1], [i, i + 1]) for i in range(4, STEPS, 2)]
+        runs = [[i, i + 1] for i in range(0, STEPS, 2)]
         keep_warm(sums.tile([P, CH], F32, name="idle", tag="sum3"), 6)
         sort_step(0)
         sort_step(1)
-        for n, (to_transpose, to_multiply) in enumerate(runs):
-            for i in to_transpose:
-                transpose_step(i, 2 if i >= 4 and i == to_transpose[0] else -1)
+        for n, run in enumerate(runs):
+            for i in run:
+                transpose_step(i, 2 if i > 0 and i == run[0] else -1)
                 if i == 0:
                     spread_vectors()
                     b1_all, bf_all, gamma_all, beta_all = spread
                     for r in range(ROW_TILES):
                         acc[r] = sums.tile([P, HID], F32, name="acc%d" % r, tag="sum%d" % r)
-            for i in to_multiply:
+            for i in run:
                 for part in range(2):
                     quantise_step(i, part)
-            if last not in to_multiply:
-                for i in to_multiply:
+            if last not in run:
+                for i in run:
                     for part in range(2):
                         multiply_part(i, part)
-                for i in runs[n + 1][0]:
+                for i in runs[n + 1]:
                     sort_step(i)
-            i = to_multiply[-1]
 
-            if i == 0:
+            if n == 0:
                 load_chunk(4)
                 for q in range(4):
                     nc.sync.dma_start(
@@ -378,11 +362,11 @@ def tile_embed_update_pa_k_kernel(
                     in_=Wf_words[0].rearrange("p n t -> p (n t)").bitcast(I32),
                 )
                 load_chunk(5)
-            if i == 3:
+            if n == 1:
                 load_chunk(6)
-            if i == 5:
+            if n == 2:
                 load_chunk(7)
-            if i == 9:
+            if n == 4:
                 nc.vector.tensor_copy(out=m_f32[:], in_=m_bf[:])
                 nc.vector.tensor_tensor(out=m_sq[:], in0=m_f32[:], in1=m_f32[:], op=ALU.mult)
                 nc.vector.tensor_scalar(
@@ -394,8 +378,8 @@ def tile_embed_update_pa_k_kernel(
             add_bias(r)
         transpose_hidden(0)
         transpose_hidden(1)
-        relu_hidden(0)
-        relu_hidden(1)
+        relu_hidden(0, True)
+        relu_hidden(1, False)
         multiply_part(last, 1)
         for r in (0, 1):
             quantise_hidden(r)
@@ -403,61 +387,65 @@ def tile_embed_update_pa_k_kernel(
         add_bias(3)
         transpose_hidden(2)
         transpose_hidden(3)
-        idle = sums.tile([P, CH], F32, name="idle", tag="sum3")
-        keep_warm(idle, 2)
+        keep_warm(sums.tile([P, CH], F32, name="idle", tag="sum3"), 2)
         score_links(0)
         score_links(1)
         link_weight(0)
-        count_links(0)
-        weighted[0] = tail.tile([P, FEAT], F32, name="weighted0")
+        link_weight(1)
         nc.vector.tensor_scalar(
-            out=weighted[0][:],
-            in0=o_sum[0][:, 0:FEAT],
-            scalar1=link_lm[:, 0:1],
+            out=pool_w[:, 0:TOKENS],
+            in0=token_of[:, 0:TOKENS],
+            scalar1=link_lm[:, 1:2],
             scalar2=None,
             op0=ALU.mult,
         )
-        relu_hidden(2)
-        relu_hidden(3)
-        link_weight(1)
-        count_links(1)
+        weighted[0] = tail.tile([P, FEAT], F32, name="weighted0")
+        nc.scalar.activation(
+            out=weighted[0][:], in_=o_sum[0][:, 0:FEAT], func=ACT.Copy, scale=link_lm[:, 0:1]
+        )
+
+        halves = [(0, HALF), (HALF, FEAT)]
+        pooled = [banks.tile([P, 4 * P], F32, name="bank") for j in range(2)]
+
+        def pool_half(j, weights, rows, opens):
+            first, last_col = halves[j]
+            nc.tensor.matmul(
+                out=pooled[j][:, 0 : last_col - first],
+                lhsT=weights[:],
+                rhs=rows[:, first:last_col],
+                start=opens,
+                stop=not opens,
+            )
+
+        relu_hidden(2, False)
+        relu_hidden(3, True)
+        o_copy = tail.tile([P, FEAT], F32)
+        nc.scalar.copy(out=o_copy[:], in_=o_sum[1][:, 0:FEAT])
         quantise_hidden(2)
         multiply_hidden(2)
         quantise_hidden(3)
         multiply_hidden(3)
         score_links(2)
         score_links(3)
-        keep_warm(banks.tile([P, CH], F32, name="bank"), 3)
-
-        halves = [(0, HALF), (HALF, FEAT)]
-        weigh(1, o_sum[1], 0, 0, FEAT)
+        for j in range(2):
+            pool_half(j, pool_w, o_copy, True)
         link_weight(2)
-        count_links(2)
-        weigh(2, o_sum[2], 1, 0, FEAT)
+        weigh(2, o_sum[2], 0, 0, FEAT)
         link_weight(3)
-        count_links(3)
+        nc.vector.tensor_tensor(out=link_ms, in0=gate[:], in1=m_f32[:], op=ALU.mult)
         nc.scalar.activation(out=warm[:], in_=eps_col[:], func=ACT.Abs_reciprocal_sqrt)
+        nc.vector.tensor_tensor(out=link_lms, in0=link_lm, in1=gate[:], op=ALU.mult)
         link_sum = banks.tile([P, 4 * P], F32, name="bank")
-        for j, cols in enumerate((link_l, link_lm, link_lms)):
-            nc.tensor.matmul(
-                out=link_sum[:, j * ROW_TILES : (j + 1) * ROW_TILES],
-                lhsT=token_of[:],
-                rhs=cols[:],
-                start=True,
-                stop=True,
-            )
-        pooled = []
-        for first, last_col in halves:
-            weigh(3, o_sum[3], 2, first, last_col)
-            half = banks.tile([P, 4 * P], F32, name="bank")
-            nc.tensor.matmul(
-                out=half[:, 0 : last_col - first],
-                lhsT=token_of[:],
-                rhs=weighted[3][:, first:last_col],
-                start=True,
-                stop=True,
-            )
-            pooled.append(half)
+        nc.tensor.matmul(
+            out=link_sum[:, 0 : 3 * ROW_TILES],
+            lhsT=token_of[:],
+            rhs=link_cols[:].rearrange("p j r -> p (j r)"),
+            start=True,
+            stop=True,
+        )
+        for j in range(2):
+            weigh(3, o_sum[3], 2, halves[j][0], halves[j][1])
+            pool_half(j, token_of, weighted[3], False)
 
         total = tail.tile([TOKENS, 3], F32)
         nc.vector.tensor_reduce(
@@ -466,33 +454,37 @@ def tile_embed_update_pa_k_kernel(
             axis=AXIS.X,
             op=ALU.add,
         )
+        biased = tail.tile([TOKENS, FEAT], F32)
+
+        def add_output_bias(j):
+            first, last = halves[j]
+            nc.vector.scalar_tensor_tensor(
+                out=biased[:, first:last],
+                in0=bf_all[0:TOKENS, first:last],
+                scalar=total[:, 1:2],
+                in1=pooled[j][0:TOKENS, 0 : last - first],
+                op0=ALU.mult,
+                op1=ALU.add,
+            )
+
+        norm = tail.tile([TOKENS, 1], F32)
+        nc.vector.tensor_scalar_add(out=norm[:], in0=total[:, 0:1], scalar1=LINKS * LINK_EPS)
         inv = tail.tile([TOKENS, 1], F32)
-        nc.vector.reciprocal(out=inv[:], in_=total[:, 0:1])
+        nc.vector.reciprocal(out=inv[:], in_=norm[:])
+        add_output_bias(0)
         gain = tail.tile([TOKENS, 1], F32)
         nc.vector.tensor_scalar(
             out=gain[:], in0=total[:, 2:3], scalar1=inv[:], scalar2=inv[:], op0=ALU.mult, op1=ALU.mult
         )
-        bias_gain = tail.tile([TOKENS, 1], F32)
-        nc.vector.tensor_scalar(
-            out=bias_gain[:], in0=total[:, 1:2], scalar1=gain[:], scalar2=None, op0=ALU.mult
-        )
-        base = tail.tile([TOKENS, FEAT], F32)
-        nc.vector.scalar_tensor_tensor(
-            out=base[:],
-            in0=bf_all[0:TOKENS, 0:FEAT],
-            scalar=bias_gain[:],
-            in1=emb[:],
-            op0=ALU.mult,
-            op1=ALU.add,
-        )
+        add_output_bias(1)
         e = tail.tile([TOKENS, FEAT], F32)
         stats = tail.tile([TOKENS, 2, 6], F32)
-        for j, (first, last) in enumerate(halves):
+        for first, last in halves:
             nc.vector.scalar_tensor_tensor(
                 out=e[:, first:last],
-                in0=pooled[j][0:TOKENS, 0 : last - first],
+                in0=biased[:, first:last],
                 scalar=gain[:],
-                in1=base[:, first:last],
+                in1=emb[:, first:last],
                 op0=ALU.mult,
                 op1=ALU.add,
             )

from contextlib import ExitStack

import concourse.mybir as mybir
from concourse.masks import make_identity

F32 = mybir.dt.float32
BF16 = mybir.dt.bfloat16
I32 = mybir.dt.int32
U32 = mybir.dt.uint32
U8 = mybir.dt.uint8
FP8X4 = mybir.dt.float8_e4m3fn_x4
ALU = mybir.AluOpType
ACT = mybir.ActivationFunctionType
AXIS = mybir.AxisListType

P = 128
ROWS = 512
ROW_TILES = ROWS // P
TOKENS = 32
LINKS = ROWS // TOKENS
LINK_PARTS = P // TOKENS
K_IN = 16384
K_PASS = 512
GROUPS = K_IN // K_PASS
HID = 512
CH = 512
FEAT = CH - 1
PAIR_WORDS = K_PASS // 2
UNITS = 8
CALL_UNITS = 4
CHUNK_GROUPS = 4
CHUNKS = GROUPS // CHUNK_GROUPS
CHUNK_K = CHUNK_GROUPS * K_PASS
STEPS = GROUPS * ROW_TILES // UNITS
X_BUFS = 10
W_BUFS = 5
HALF = 256
LN_EPS = 1e-5
LINK_EPS = 1e-8

FLOPS = 2 * ROWS * K_IN * HID + 2 * ROWS * HID * CH


def tile_embed_update_pa_k_kernel(
    tc, net_in, embeds, m, W1_words, W1_scales, b1, Wf_words, Wf_scales, b_f, gamma, beta, out
):
    nc = tc.nc
    x_dram = net_in.rearrange("b s k i -> (b s k) i").rearrange("(p r) i -> p r i", r=ROW_TILES)
    w1_dram = W1_words.rearrange("g p n t -> p g (n t)").bitcast(I32)

    with ExitStack() as ctx:
        ctx.enter_context(tc.manual_schedule())
        consts = ctx.enter_context(tc.tile_pool(name="consts", bufs=1))
        loads = ctx.enter_context(tc.tile_pool(name="loads", bufs=1))
        work = ctx.enter_context(tc.tile_pool(name="work", bufs=2))
        tail = ctx.enter_context(tc.tile_pool(name="tail", bufs=1))
        sums = ctx.enter_context(tc.psum_pool(name="sums", bufs=1))
        banks = ctx.enter_context(tc.psum_pool(name="banks", bufs=4))

        vecs = consts.tile([P, CH], BF16)
        nc.vector.memset(vecs[:].bitcast(I32), 0)
        w1_planes = consts.tile([P, CHUNKS, HID], U8, align_bytes=256)
        nc.vector.memset(w1_planes[:, 0, :].bitcast(I32), 0)
        zero_rows = consts.tile([P, CH], BF16)
        nc.vector.memset(zero_rows[:].bitcast(I32), 0)
        zero_col = consts.tile([P, 1], F32)
        nc.vector.memset(zero_col[:], 0.0)
        ident_f32 = consts.tile([P, P], F32)
        make_identity(nc, ident_f32[:])
        ident_bf = consts.tile([P, P], BF16)
        nc.vector.tensor_copy(out=ident_bf[:], in_=ident_f32[:])
        eps_col = consts.tile([P, 1], F32)
        nc.vector.tensor_scalar(
            out=eps_col[:], in0=zero_col[:], scalar1=1.0, scalar2=LN_EPS, op0=ALU.mult, op1=ALU.add
        )
        nc.vector.memset(w1_planes[:, 1:CHUNKS, :].bitcast(I32), 0)
        wf_plane = consts.tile([P, CH], U8, align_bytes=256)
        nc.gpsimd.memset(wf_plane[:].bitcast(I32), 0)
        token_of = consts.tile([P, P], F32)
        nc.gpsimd.memset(token_of[:], 0.0)
        pool_w = consts.tile([P, P], F32)
        nc.gpsimd.memset(pool_w[:], 0.0)

        nc.scalar.dma_start(out=vecs[0:1, 0:HID], in_=b1.rearrange("(o n) -> o n", o=1))
        nc.scalar.dma_start(out=vecs[1:2, 0:CH], in_=b_f.rearrange("(o n) -> o n", o=1))
        nc.scalar.dma_start(out=vecs[2:3, 0:FEAT], in_=gamma.rearrange("(o n) -> o n", o=1))
        nc.scalar.dma_start(out=vecs[3:4, 0:FEAT], in_=beta.rearrange("(o n) -> o n", o=1))

        warm = consts.tile([P, 1], F32)
        nc.scalar.activation(out=warm[:], in_=zero_col[:], func=ACT.Sigmoid)

        x_place = {}
        w_place = {}

        def load_x(c, tiles):
            x_raw = loads.tile([P, len(tiles), CHUNK_K], BF16, name="x_raw", bufs=X_BUFS)
            nc.sync.dma_start(
                out=x_raw[:],
                in_=x_dram[:, tiles[0] : tiles[-1] + 1, c * CHUNK_K : (c + 1) * CHUNK_K],
            )
            for place, r in enumerate(tiles):
                x_place[r, c] = x_raw[:, place, :]

        def load_scales(c):
            for q in range(4):
                nc.sync.dma_start(
                    out=w1_planes[32 * q : 32 * q + 16, c, :].bitcast(I32),
                    in_=W1_scales[
                        c * CHUNK_GROUPS : (c + 1) * CHUNK_GROUPS, 4 * q : 4 * q + 4, :
                    ].bitcast(I32),
                )

        def load_w(first, groups):
            whole = groups == CHUNK_GROUPS
            w_words = loads.tile(
                [P, groups, HID],
                U32,
                name="w_words",
                tag="w_chunk" if whole else "w_part",
                bufs=W_BUFS if whole else 2,
                align_bytes=256,
            )
            nc.sync.dma_start(out=w_words[:].bitcast(I32), in_=w1_dram[:, first : first + groups, :])
            for g in range(groups):
                w_place[first + g] = w_words[:, g, :]

        def load_chunk(c):
            load_x(c, [0, 1])
            load_x(c, [2, 3])
            load_scales(c)
            load_w(c * CHUNK_GROUPS, CHUNK_GROUPS)

        for r in range(ROW_TILES):
            load_x(0, [r])
        load_scales(0)
        load_w(0, CHUNK_GROUPS // 2)
        load_w(CHUNK_GROUPS // 2, CHUNK_GROUPS // 2)
        for c in range(1, 4):
            load_chunk(c)
        m_bf = consts.tile([P, ROW_TILES], BF16)
        nc.sync.dma_start(
            out=m_bf[:], in_=m.rearrange("b s k o -> (b s k o)").rearrange("(p r) -> p r", r=ROW_TILES)
        )
        emb = consts.tile([TOKENS, FEAT], BF16)
        nc.sync.dma_start(out=emb[:], in_=embeds.rearrange("b s c -> (b s) c"))

        nc.vector.tensor_reduce(
            out=token_of[:, 0:TOKENS],
            in_=ident_f32[:].rearrange("p (j i) -> p j i", i=LINK_PARTS),
            axis=AXIS.X,
            op=ALU.add,
        )
        spread = []

        def spread_vectors():
            for j in range(4):
                picked = sums.tile([P, CH], F32, name="picked", tag="sum%d" % j)
                nc.tensor.matmul(
                    out=picked[:],
                    lhsT=ident_bf[:, j : j + 1].to_broadcast([P, P]),
                    rhs=vecs[:],
                    start=True,
                    stop=True,
                )
                row = consts.tile([P, CH], F32, name="spread%d" % j)
                nc.scalar.copy(out=row[:], in_=picked[:])
                spread.append(row)

        def keep_warm(idle, count):
            for j in range(count):
                nc.tensor.matmul(out=idle[:], lhsT=ident_bf[:], rhs=zero_rows[:], start=True, stop=True)

        acc = {}
        sorted_tiles = {}
        grouped_tiles = {}

        def parts_of(i):
            return [(i % 2 * 2 + r, i // 2) for r in range(2)]

        def units_of(i):
            return [(r, c * CHUNK_GROUPS + g) for r, c in parts_of(i) for g in range(CHUNK_GROUPS)]

        def sort_step(i):
            x_sorted = work.tile([P, UNITS, 2, P], F32, name="x_sorted")
            for half, part in enumerate(parts_of(i)):
                nc.vector.tensor_copy(
                    out=x_sorted[:, half * CHUNK_GROUPS : (half + 1) * CHUNK_GROUPS, :, :],
                    in_=x_place[part]
                    .bitcast(F32)
                    .rearrange("p (g q u) -> p g u q", u=2, q=P),
                )
            sorted_tiles[i] = x_sorted

        def transpose_step(i, vector_bank):
            x_sorted = sorted_tiles[i]
            grouped = work.tile([P, UNITS, K_PASS], BF16, name="grouped", align_bytes=256)
            grouped_words = grouped[:].bitcast(F32)
            for k in range(0, UNITS, 2):
                bank = banks.tile([P, 4 * P], F32, name="bank")
                for k2 in range(2):
                    for u in range(2):
                        nc.tensor.transpose(
                            bank[:, (2 * k2 + u) * P : (2 * k2 + u + 1) * P],
                            x_sorted[:, k + k2, u, :],
                            ident_f32[:],
                        )
                words_out = grouped_words[:, k : k + 2, :].rearrange("p k (j u) -> p k j u", u=2)
                words_in = bank[:].rearrange("p (k u j) -> p k j u", k=2, u=2)
                if k // 2 == vector_bank:
                    nc.vector.tensor_copy(out=words_out, in_=words_in)
                else:
                    nc.scalar.copy(out=words_out, in_=words_in)
            grouped_tiles[i] = grouped

        code_tiles = {}

        def quantise_step(i, part):
            if part == 0:
                x_codes = work.tile([P, UNITS, P], U32, name="x_codes", align_bytes=256)
                x_planes = work.tile([P, UNITS, P], U8, name="x_planes", align_bytes=256)
                code_tiles[i] = (x_codes, x_planes)
            x_codes, x_planes = code_tiles[i]
            units = slice(part * CALL_UNITS, (part + 1) * CALL_UNITS)
            nc.vector.quantize_mx(
                out=x_codes[:, units, :].rearrange("p k j -> p (k j)").bitcast(FP8X4),
                scales=x_planes[:, units, :].rearrange("p k j -> p (k j)"),
                in_=grouped_tiles[i][:, units, :].rearrange("p k j -> p (k j)"),
            )

        def multiply_part(i, part):
            x_codes, x_planes = code_tiles[i]
            for k in range(part * CHUNK_GROUPS, (part + 1) * CHUNK_GROUPS):
                r, group = units_of(i)[k]
                c, j = divmod(group, CHUNK_GROUPS)
                nc.tensor.matmul_mx(
                    out=acc[r][:],
                    lhsT=x_codes[:, k, :].bitcast(FP8X4),
                    lhsT_scale=x_planes[:, k, :],
                    rhs=w_place[group].bitcast(FP8X4),
                    rhs_scale=w1_planes[4 * j : P, c, :],
                    start=(group == 0),
                    stop=(group == GROUPS - 1),
                )

        wf_words = consts.tile([P, CH], U32, align_bytes=256)
        pre_h = tail.tile([P, ROW_TILES, HID], BF16)
        h_grouped = tail.tile([P, ROW_TILES, HID], BF16, align_bytes=64)
        h_codes = tail.tile([P, ROW_TILES, P], U32, align_bytes=64)
        h_planes = tail.tile([P, ROW_TILES, P], U8, align_bytes=64)
        gate = tail.tile([P, ROW_TILES], F32)
        link_cols = tail.tile([P, 3, ROW_TILES], F32)
        link_ms, link_lm, link_lms = [link_cols[:, j, :] for j in range(3)]
        m_f32 = consts.tile([P, ROW_TILES], F32)
        m_sq = consts.tile([P, ROW_TILES], F32)
        m_eps = consts.tile([P, ROW_TILES], F32)
        o_sum = {}

        def add_bias(r):
            nc.vector.tensor_tensor(out=pre_h[:, r, :], in0=acc[r][:], in1=spread[0][:], op=ALU.add)

        hidden_banks = {}

        def transpose_hidden(r):
            pre_h_words = pre_h[:].bitcast(F32)
            bank = banks.tile([P, 4 * P], F32, name="bank")
            for u in range(2):
                nc.tensor.transpose(
                    bank[:, u * P : (u + 1) * P], pre_h_words[:, r, u : PAIR_WORDS : 2], ident_f32[:]
                )
            hidden_banks[r] = bank

        def relu_hidden(r, on_scalar):
            h_out = h_grouped[:, r, :].rearrange("p (j u e) -> p j u e", u=2, e=2)
            h_in = hidden_banks[r][:, 0 : 2 * P].bitcast(BF16).rearrange("p (u j e) -> p j u e", u=2, e=2)
            if on_scalar:
                nc.scalar.activation(out=h_out, in_=h_in, func=ACT.Relu)
            else:
                nc.vector.tensor_scalar(out=h_out, in0=h_in, scalar1=0.0, scalar2=None, op0=ALU.max)

        def quantise_hidden(r):
            nc.vector.quantize_mx(
                out=h_codes[:, r, :].bitcast(FP8X4), scales=h_planes[:, r, :], in_=h_grouped[:, r, :]
            )

        def multiply_hidden(r):
            o_ps = sums.tile([P, CH], F32, name="o_ps", tag="sum%d" % r)
            nc.tensor.matmul_mx(
                out=o_ps[:],
                lhsT=h_codes[:, r, :].bitcast(FP8X4),
                lhsT_scale=h_planes[:, r, :],
                rhs=wf_words[:].bitcast(FP8X4),
                rhs_scale=wf_plane[:],
                start=True,
                stop=True,
            )
            o_sum[r] = o_ps

        def score_links(r):
            nc.scalar.activation(
                out=gate[:, r : r + 1],
                in_=o_sum[r][:, FEAT:CH],
                func=ACT.Sigmoid,
                bias=spread[1][:, FEAT:CH],
            )

        def link_weight(r):
            nc.vector.tensor_scalar(
                out=link_lm[:, r : r + 1],
                in0=gate[:, r : r + 1],
                scalar1=m_sq[:, r : r + 1],
                scalar2=m_eps[:, r : r + 1],
                op0=ALU.mult,
                op1=ALU.add,
            )

        weighted = {}

        def weigh(r, o, onto, first, last):
            if first == 0:
                weighted[r] = tail.tile([P, FEAT], F32, name="weighted%d" % r)
            nc.vector.scalar_tensor_tensor(
                out=weighted[r][:, first:last],
                in0=o[:, first:last],
                scalar=link_lm[:, r : r + 1],
                in1=weighted[onto][:, first:last],
                op0=ALU.mult,
                op1=ALU.add,
            )

        last = STEPS - 1
        runs = [[i, i + 1] for i in range(0, STEPS, 2)]
        keep_warm(sums.tile([P, CH], F32, name="idle", tag="sum3"), 6)
        sort_step(0)
        sort_step(1)
        for n, run in enumerate(runs):
            for i in run:
                transpose_step(i, 2 if i > 0 and i == run[0] else -1)
                if i == 0:
                    spread_vectors()
                    b1_all, bf_all, gamma_all, beta_all = spread
                    for r in range(ROW_TILES):
                        acc[r] = sums.tile([P, HID], F32, name="acc%d" % r, tag="sum%d" % r)
            for i in run:
                for part in range(2):
                    quantise_step(i, part)
            if last not in run:
                for i in run:
                    for part in range(2):
                        multiply_part(i, part)
                for i in runs[n + 1]:
                    sort_step(i)

            if n == 0:
                load_chunk(4)
                for q in range(4):
                    nc.sync.dma_start(
                        out=wf_plane[32 * q : 32 * q + 4, :].bitcast(I32),
                        in_=Wf_scales[0, 4 * q : 4 * q + 4, :].bitcast(I32),
                    )
                nc.sync.dma_start(
                    out=wf_words[:].bitcast(I32),
                    in_=Wf_words[0].rearrange("p n t -> p (n t)").bitcast(I32),
                )
                load_chunk(5)
            if n == 1:
                load_chunk(6)
            if n == 2:
                load_chunk(7)
            if n == 4:
                nc.vector.tensor_copy(out=m_f32[:], in_=m_bf[:])
                nc.vector.tensor_tensor(out=m_sq[:], in0=m_f32[:], in1=m_f32[:], op=ALU.mult)
                nc.vector.tensor_scalar(
                    out=m_eps[:], in0=m_f32[:], scalar1=LINK_EPS, scalar2=None, op0=ALU.mult
                )

        for r in range(3):
            multiply_part(last - 1 + r // 2, r % 2)
            add_bias(r)
        transpose_hidden(0)
        transpose_hidden(1)
        relu_hidden(0, True)
        relu_hidden(1, False)
        multiply_part(last, 1)
        for r in (0, 1):
            quantise_hidden(r)
            multiply_hidden(r)
        add_bias(3)
        transpose_hidden(2)
        transpose_hidden(3)
        keep_warm(sums.tile([P, CH], F32, name="idle", tag="sum3"), 2)
        score_links(0)
        score_links(1)
        link_weight(0)
        link_weight(1)
        nc.vector.tensor_scalar(
            out=pool_w[:, 0:TOKENS],
            in0=token_of[:, 0:TOKENS],
            scalar1=link_lm[:, 1:2],
            scalar2=None,
            op0=ALU.mult,
        )
        weighted[0] = tail.tile([P, FEAT], F32, name="weighted0")
        nc.scalar.activation(
            out=weighted[0][:], in_=o_sum[0][:, 0:FEAT], func=ACT.Copy, scale=link_lm[:, 0:1]
        )

        halves = [(0, HALF), (HALF, FEAT)]
        pooled = [banks.tile([P, 4 * P], F32, name="bank") for j in range(2)]

        def pool_half(j, weights, rows, opens):
            first, last_col = halves[j]
            nc.tensor.matmul(
                out=pooled[j][:, 0 : last_col - first],
                lhsT=weights[:],
                rhs=rows[:, first:last_col],
                start=opens,
                stop=not opens,
            )

        relu_hidden(2, False)
        relu_hidden(3, True)
        o_copy = tail.tile([P, FEAT], F32)
        nc.scalar.copy(out=o_copy[:], in_=o_sum[1][:, 0:FEAT])
        quantise_hidden(2)
        multiply_hidden(2)
        quantise_hidden(3)
        multiply_hidden(3)
        score_links(2)
        score_links(3)
        for j in range(2):
            pool_half(j, pool_w, o_copy, True)
        link_weight(2)
        weigh(2, o_sum[2], 0, 0, FEAT)
        link_weight(3)
        nc.vector.tensor_tensor(out=link_ms, in0=gate[:], in1=m_f32[:], op=ALU.mult)
        nc.scalar.activation(out=warm[:], in_=eps_col[:], func=ACT.Abs_reciprocal_sqrt)
        nc.vector.tensor_tensor(out=link_lms, in0=link_lm, in1=gate[:], op=ALU.mult)
        link_sum = banks.tile([P, 4 * P], F32, name="bank")
        nc.tensor.matmul(
            out=link_sum[:, 0 : 3 * ROW_TILES],
            lhsT=token_of[:],
            rhs=link_cols[:].rearrange("p j r -> p (j r)"),
            start=True,
            stop=True,
        )
        for j in range(2):
            weigh(3, o_sum[3], 2, halves[j][0], halves[j][1])
            pool_half(j, token_of, weighted[3], False)

        total = tail.tile([TOKENS, 3], F32)
        nc.vector.tensor_reduce(
            out=total[:],
            in_=link_sum[0:TOKENS, 0 : 3 * ROW_TILES].rearrange("p (j r) -> p j r", r=ROW_TILES),
            axis=AXIS.X,
            op=ALU.add,
        )
        biased = tail.tile([TOKENS, FEAT], F32)

        def add_output_bias(j):
            first, last = halves[j]
            nc.vector.scalar_tensor_tensor(
                out=biased[:, first:last],
                in0=bf_all[0:TOKENS, first:last],
                scalar=total[:, 1:2],
                in1=pooled[j][0:TOKENS, 0 : last - first],
                op0=ALU.mult,
                op1=ALU.add,
            )

        norm = tail.tile([TOKENS, 1], F32)
        nc.vector.tensor_scalar_add(out=norm[:], in0=total[:, 0:1], scalar1=LINKS * LINK_EPS)
        inv = tail.tile([TOKENS, 1], F32)
        nc.vector.reciprocal(out=inv[:], in_=norm[:])
        add_output_bias(0)
        gain = tail.tile([TOKENS, 1], F32)
        nc.vector.tensor_scalar(
            out=gain[:], in0=total[:, 2:3], scalar1=inv[:], scalar2=inv[:], op0=ALU.mult, op1=ALU.mult
        )
        add_output_bias(1)
        e = tail.tile([TOKENS, FEAT], F32)
        stats = tail.tile([TOKENS, 2, 6], F32)
        for first, last in halves:
            nc.vector.scalar_tensor_tensor(
                out=e[:, first:last],
                in0=biased[:, first:last],
                scalar=gain[:],
                in1=emb[:, first:last],
                op0=ALU.mult,
                op1=ALU.add,
            )
        for j, (first, last) in enumerate(halves):
            nc.vector.bn_stats(out=stats[:, j, :], in_=e[:, first:last])
        mean_var = tail.tile([TOKENS, 2], F32)
        nc.vector.bn_aggr(out=mean_var[:], in_=stats[:].rearrange("p j s -> p (j s)"))
        rstd = tail.tile([TOKENS, 1], F32)
        nc.scalar.activation(
            out=rstd[:],
            in_=mean_var[:, 1:2],
            func=ACT.Abs_reciprocal_sqrt,
            bias=eps_col[0:TOKENS, :],
        )
        centred = tail.tile([TOKENS, FEAT], F32)
        for first, last in halves:
            nc.vector.scalar_tensor_tensor(
                out=centred[:, first:last],
                in0=e[:, first:last],
                scalar=mean_var[:, 0:1],
                in1=gamma_all[0:TOKENS, first:last],
                op0=ALU.subtract,
                op1=ALU.mult,
            )
        y = tail.tile([TOKENS, FEAT], F32)
        for first, last in halves:
            nc.vector.scalar_tensor_tensor(
                out=y[:, first:last],
                in0=centred[:, first:last],
                scalar=rstd[:],
                in1=beta_all[0:TOKENS, first:last],
                op0=ALU.mult,
                op1=ALU.add,
            )
        nc.sync.dma_start(out=out.rearrange("b s c -> (b s) c"), in_=y[:])
